import numpy as np
import ml_dtypes


def mxq(x, axis, fmt="e4m3"):
    dtype, down = {"e4m3": (ml_dtypes.float8_e4m3fn, 7), "e5m2": (ml_dtypes.float8_e5m2, 14)}[fmt]
    v = np.moveaxis(np.asarray(x, np.float32).astype(ml_dtypes.bfloat16).astype(np.float64), axis, -1)
    blocks = v.reshape(v.shape[:-1] + (-1, 32))
    amax = np.abs(blocks).max(-1, keepdims=True)
    byte = np.maximum(np.where(amax > 0, np.frexp(amax)[1] - 1 + 127, 0) - down, 1)
    scale = np.exp2(byte - 127.0)
    codes = (blocks / scale).astype(np.float32).astype(dtype).astype(np.float64)
    return np.moveaxis((codes * scale).reshape(v.shape), -1, axis)


WIDE = False


def mx_kscale(k):
    if not WIDE:
        return np.ones(k)
    levels = np.array([10, -10, 5, -5, 0])
    a = np.random.permutation(np.resize(levels, k // 512 * 4)).reshape(k // 512, 4)
    idx = np.arange(k)
    return np.exp2(a[idx // 512, idx % 128 // 32])


BF16 = ml_dtypes.bfloat16


def bf(x):
    return np.asarray(x, np.float32).astype(BF16)


def f64(x):
    return np.asarray(x).astype(np.float64)


E2M1 = np.array([0.0, 0.5, 1.0, 1.5, 2.0, 3.0, 4.0, 6.0, -0.0, -0.5, -1.0, -1.5, -2.0, -3.0, -4.0, -6.0])


def pack_weight(w, fmt):
    k, n = w.shape
    w = f64(bf(w)).reshape(k // 32, 32, n)
    amax = np.abs(w).max(1)
    if fmt == "e4m3":
        byte = np.frexp(amax)[1] - 1 + 127 - 7
    else:
        mant, ex = np.frexp(amax / 6.0)
        byte = np.where(mant > 0.5, ex, ex - 1) + 127
    byte = np.clip(np.where(amax > 0, byte, 1), 1, 254)
    scaled = (w * np.exp2(127.0 - byte)[:, None, :]).reshape(k, n).astype(np.float32)
    by_word = np.ascontiguousarray(scaled.reshape(k // 512, 128, 4, n).transpose(0, 1, 3, 2))
    if fmt == "e4m3":
        words = by_word.astype(ml_dtypes.float8_e4m3fn).view(np.uint8)
    else:
        c = by_word.astype(ml_dtypes.float4_e2m1fn).view(np.uint8) & 0xF
        words = c[..., 0::2] | (c[..., 1::2] << 4)
    return np.ascontiguousarray(words), np.ascontiguousarray(byte.astype(np.uint8).reshape(k // 512, 16, n))


def unpack_weight(words, scales, fmt):
    g, p, n, _ = words.shape
    if fmt == "e4m3":
        vals = np.ascontiguousarray(words).view(ml_dtypes.float8_e4m3fn).astype(np.float64)
    else:
        nib = np.empty((g, p, n, 4), np.uint8)
        nib[..., 0::2] = words & 0xF
        nib[..., 1::2] = words >> 4
        vals = E2M1[nib]
    vals = vals * np.repeat(np.exp2(scales.astype(np.float64) - 127.0), 8, axis=1)[..., None]
    return vals.transpose(0, 1, 3, 2).reshape(g * 512, n)


B, F, C, DEPTH, LQ = 512, 8192, 1024, 11, 7
NL = 2 ** (DEPTH - 1)
NQ = 2 ** LQ


def sigmoid(v):
    return 1.0 / (1.0 + np.exp(-v))


def setup_inputs():
    s = mx_kscale(F)
    x = bf(np.random.standard_normal((B, F)) * s)
    W_gate = bf(np.random.standard_normal((F, NL - 1)) * 2.0 / np.sqrt(F) / s[:, None])
    b_gate = bf(np.random.standard_normal(NL - 1) * 0.5)
    words, scales = pack_weight(np.random.standard_normal((NL, C)) * 0.5 * 1.2 ** (DEPTH - 1), "e4m3")
    return {"x": x,
            "W_gate": W_gate,
            "b_gate": b_gate,
            "leaf_logits_words": words,
            "leaf_logits_scales": scales}


def reference(x, W_gate, b_gate, leaf_logits_words, leaf_logits_scales):
    nb = x.shape[0]
    xf, wf = f64(x), f64(W_gate)
    top = (xf @ wf[:, :NQ])[:, :NQ - 1]
    low = mxq(xf, 1, "e4m3") @ mxq(wf[:, NQ - 1:], 0, "e4m3")
    p = sigmoid(np.concatenate([top, low], axis=1) + f64(b_gate))
    probs = np.ones((nb, 1))
    for level in range(DEPTH - 1):
        n = 2 ** level
        start = n - 1
        pl = p[:, start:start + n]
        probs = np.stack([(1.0 - pl) * probs, pl * probs], axis=-1).reshape(nb, 2 * n)
    return mxq(probs, 1, "e4m3") @ unpack_weight(leaf_logits_words, leaf_logits_scales, "e4m3")

@@ -1,0 +1,325 @@
+import concourse.mybir as mybir
+from concourse.masks import make_identity
+
+F32 = mybir.dt.float32
+BF16 = mybir.dt.bfloat16
+I32 = mybir.dt.int32
+U32 = mybir.dt.uint32
+U8 = mybir.dt.uint8
+FP8X4 = mybir.dt.float8_e4m3fn_x4
+SIGMOID = mybir.ActivationFunctionType.Sigmoid
+MULT = mybir.AluOpType.mult
+
+P = 128
+BATCH = 512
+FEATURES = 8192
+NODES = 1023
+CLASSES = 1024
+BATCH_TILES = BATCH // P
+K_PASS = 4 * P
+PASSES = FEATURES // K_PASS
+X_COLS = 2048
+PASSES_PER_X = X_COLS // K_PASS
+N_TILE = 512
+
+FIRST_7 = 127
+FIRST_9 = 511
+LATE_RUN = 8
+
+FLOPS = 2 * BATCH * FEATURES * NODES + 2 * BATCH * CLASSES * CLASSES
+
+
+def tile_treemodel_k_kernel(tc, x, W_gate, b_gate, leaf_logits_words, leaf_logits_scales, out):
+    nc = tc.nc
+    with tc.tile_pool(name="keep", bufs=1) as keep, tc.psum_pool(name="psum", bufs=1) as psum:
+
+        def bank(index, shape, name):
+            return psum.tile(shape, F32, name=name, tag="bank%d" % index)
+
+        ident = keep.tile([P, P], F32, name="ident")
+        make_identity(nc, ident[:])
+
+        leaf_codes = keep.tile([P, 2, 4 * CLASSES], U8, name="leaf_codes", align_bytes=64)
+        leaf_scales = keep.tile([P, 2, CLASSES], U8, name="leaf_scales", align_bytes=64)
+        nc.vector.memset(leaf_scales[:].bitcast(I32), 0)
+
+        rows_plain = keep.tile([P, P], BF16, name="rows_plain")
+        rows_every_2nd = keep.tile([P, 2 * P], BF16, name="rows_every_2nd")
+        nc.vector.memset(rows_plain[:], 0.0)
+        nc.vector.memset(rows_every_2nd[:], 0.0)
+        nc.scalar.dma_start(out=rows_plain[0:1, :], in_=b_gate[0:P].unsqueeze(0))
+        nc.scalar.dma_start(
+            out=rows_plain[1:4, :], in_=b_gate[FIRST_7:FIRST_9].rearrange("(r n) -> r n", r=3)
+        )
+        nc.scalar.dma_start(
+            out=rows_every_2nd[0:2, :], in_=b_gate[FIRST_9:NODES].rearrange("(r n) -> r n", r=2)
+        )
+        nc.scalar.dma_start(
+            out=rows_every_2nd[2:3, :], in_=b_gate[FIRST_9 + 1 : FIRST_9 + 1 + 2 * P].unsqueeze(0)
+        )
+        nc.scalar.dma_start(
+            out=rows_every_2nd[3:4, 0 : 2 * P - 1], in_=b_gate[FIRST_9 + 1 + 2 * P : NODES].unsqueeze(0)
+        )
+        rows_f32 = keep.tile([P, 2, P], F32, name="rows_f32")
+        nc.vector.tensor_copy(out=rows_f32[:, 0, :], in_=rows_plain[:])
+        nc.vector.tensor_copy(
+            out=rows_f32[:, 1, :], in_=rows_every_2nd[:].rearrange("p (m two) -> p m two", two=2)[:, :, 0]
+        )
+        bias_ps = bank(6, [P, 2, P], "bias_ps")
+        for i in range(2):
+            nc.tensor.transpose(bias_ps[:, i, :], rows_f32[:, i, :], ident[:])
+        bias = keep.tile([P, 2, 4], F32, name="bias")
+        neg_bias = keep.tile([P, 2, 4], F32, name="neg_bias")
+        nc.vector.tensor_copy(out=bias[:], in_=bias_ps[:, :, 0:4])
+        nc.vector.tensor_scalar_mul(out=neg_bias[:], in0=bias[:], scalar1=-1.0)
+
+        x_codes = keep.tile([P, PASSES, BATCH], U32, name="x_codes", align_bytes=64)
+        x_scales = keep.tile([P, PASSES, BATCH], U8, name="x_scales", align_bytes=64)
+        late_codes = keep.tile([P, PASSES, 2 * P], U32, name="late_codes", align_bytes=64)
+        late_scales = keep.tile([P, PASSES, 2 * P], U8, name="late_scales", align_bytes=64)
+
+        acc_top = bank(0, [P, BATCH], "acc_top")
+        acc_7 = bank(1, [P, BATCH], "acc_7")
+        acc_8 = [bank(2 + h, [P, BATCH], "acc_8_%d" % h) for h in range(2)]
+        acc_9 = {(0, u): bank(4 + u, [P, BATCH], "acc_9_0_%d" % u) for u in range(2)}
+
+        streamed = [(acc_9[(0, 0)], 0), (acc_9[(0, 1)], P), (acc_7, 2 * P), (acc_8[0], 3 * P), (acc_8[1], 4 * P)]
+
+        with tc.tile_pool(name="x_raw", bufs=2 * BATCH_TILES) as x_pool, tc.tile_pool(
+            name="w_raw", bufs=4
+        ) as w_pool, tc.tile_pool(name="stage", bufs=2) as stage, tc.tile_pool(
+            name="codes", bufs=3
+        ) as codes_pool, tc.manual_schedule():
+            x_raw = {}
+            ready = {}
+
+            def load_x(block, bt):
+                piece = x_pool.tile([P, X_COLS], BF16, name="x_piece")
+                nc.sync.dma_start(
+                    out=piece[:], in_=x[bt * P : (bt + 1) * P, block * X_COLS : (block + 1) * X_COLS]
+                )
+                x_raw[(block, bt)] = piece
+
+            def prepare(c):
+                block, c_in_block = divmod(c, PASSES_PER_X)
+                w_raw = w_pool.tile([P, 4, NODES], BF16, name="w_raw")
+                nc.sync.dma_start(
+                    out=w_raw[:].rearrange("p (u e) n -> p u e n", u=2),
+                    in_=W_gate[c * K_PASS : (c + 1) * K_PASS, :].rearrange("(u p e) n -> p u e n", u=2, p=P),
+                )
+                if block + 1 < FEATURES // X_COLS:
+                    load_x(block + 1, c_in_block)
+
+                xt_ps = [bank(6 + u, [P, BATCH], "xt_ps%d" % u) for u in range(2)]
+                for u in range(2):
+                    for bt in range(BATCH_TILES):
+                        first = (2 * c_in_block + u) * P
+                        nc.tensor.transpose(
+                            xt_ps[u][:, bt * P : (bt + 1) * P],
+                            x_raw[(block, bt)][:].bitcast(F32)[:, first : first + P],
+                            ident[:],
+                        )
+                x_t = stage.tile([P, 2, BATCH], F32, name="x_t")
+                for u in range(2):
+                    nc.scalar.copy(out=x_t[:, u, :], in_=xt_ps[u][:])
+
+                w_grouped = stage.tile([P, 7 * P, 4], BF16, name="w_grouped", align_bytes=64)
+                for h in range(2):
+                    first = FIRST_9 + 2 * P * h
+                    nc.vector.tensor_copy(
+                        out=w_grouped[:, 2 * P * h : 2 * P * (h + 1), :].rearrange("p (u m) t -> p u m t", u=2),
+                        in_=w_raw[:, :, first : first + 2 * P].rearrange("p t (m u) -> p u m t", u=2),
+                    )
+                nc.scalar.copy(
+                    out=w_grouped[:, 4 * P : 7 * P, :],
+                    in_=w_raw[:, :, FIRST_7:FIRST_9].rearrange("p t n -> p n t"),
+                )
+                x_grouped = stage.tile([P, BATCH, 2], F32, name="x_grouped", align_bytes=64)
+                nc.vector.tensor_copy(out=x_grouped[:], in_=x_t[:].rearrange("p u b -> p b u"))
+
+                w_codes = codes_pool.tile([P, 5 * P], U32, name="w_codes", align_bytes=64)
+                w_scales = codes_pool.tile([P, 5 * P], U8, name="w_scales", align_bytes=64)
+
+                def quantise_w(first, count, codes, scales):
+                    nc.vector.quantize_mx(
+                        out=codes.bitcast(FP8X4),
+                        scales=scales,
+                        in_=w_grouped[:, first : first + count, :].rearrange("p n t -> p (n t)"),
+                    )
+
+                quantise_w(0, 2 * P, w_codes[:, 0 : 2 * P], w_scales[:, 0 : 2 * P])
+                quantise_w(2 * P, 2 * P, late_codes[:, c, :], late_scales[:, c, :])
+                nc.vector.quantize_mx(
+                    out=x_codes[:, c, :].bitcast(FP8X4),
+                    scales=x_scales[:, c, :],
+                    in_=x_grouped[:].rearrange("p b u -> p (b u)").bitcast(BF16),
+                )
+                quantise_w(4 * P, P, w_codes[:, 2 * P : 3 * P], w_scales[:, 2 * P : 3 * P])
+                quantise_w(5 * P, 2 * P, w_codes[:, 3 * P : 5 * P], w_scales[:, 3 * P : 5 * P])
+                ready[c] = (w_raw, x_t, w_codes, w_scales)
+
+            def multiply(c):
+                w_raw, x_t, w_codes, w_scales = ready[c]
+                x_bf16 = x_t[:].bitcast(BF16).rearrange("p u (b e) -> p u b e", e=2)
+                for t in range(4):
+                    nc.tensor.matmul(
+                        out=acc_top[:],
+                        lhsT=w_raw[:, t, 0:P],
+                        rhs=x_bf16[:, t // 2, :, t % 2],
+                        start=(c == 0 and t == 0),
+                        stop=(c == PASSES - 1 and t == 3),
+                    )
+                for acc, first in streamed:
+                    nc.tensor.matmul_mx(
+                        out=acc[:],
+                        lhsT=w_codes[:, first : first + P].bitcast(FP8X4),
+                        lhsT_scale=w_scales[:, first : first + P],
+                        rhs=x_codes[:, c, :].bitcast(FP8X4),
+                        rhs_scale=x_scales[:, c, :],
+                        start=(c == 0),
+                        stop=(c == PASSES - 1),
+                    )
+
+            for bt in range(BATCH_TILES):
+                load_x(0, bt)
+            prepare(0)
+            for c in range(1, PASSES):
+                prepare(c)
+                multiply(c - 1)
+            multiply(PASSES - 1)
+
+            for q4 in range(4):
+                nc.sync.dma_start(
+                    out=leaf_scales[32 * q4 : 32 * q4 + 4, :, :].bitcast(I32),
+                    in_=leaf_logits_scales[:, 4 * q4 : 4 * q4 + 4, :].bitcast(I32).rearrange("h r n -> r h n"),
+                )
+            for h in range(2):
+                nc.sync.dma_start(
+                    out=leaf_codes[:, h, :].bitcast(I32),
+                    in_=leaf_logits_words[h].rearrange("p n t -> p (n t)").bitcast(I32),
+                )
+
+        with tc.tile_pool(name="tree", bufs=1) as tree, tc.tile_pool(name="result", bufs=2) as result:
+            for u in range(2):
+                acc_9[(1, u)] = bank(6 + u, [P, BATCH], "acc_9_1_%d" % u)
+
+            def late_run(run):
+                for i in range(run * LATE_RUN, (run + 1) * LATE_RUN):
+                    u, c = divmod(i, PASSES)
+                    nc.tensor.matmul_mx(
+                        out=acc_9[(1, u)][:],
+                        lhsT=late_codes[:, c, u * P : (u + 1) * P].bitcast(FP8X4),
+                        lhsT_scale=late_scales[:, c, u * P : (u + 1) * P],
+                        rhs=x_codes[:, c, :].bitcast(FP8X4),
+                        rhs_scale=x_scales[:, c, :],
+                        start=(c == 0),
+                        stop=(c == PASSES - 1),
+                    )
+
+            def branches(dst, acc, row, col):
+                nc.scalar.activation(
+                    out=dst[:, 1, :], in_=acc[:], func=SIGMOID, bias=bias[:, row, col : col + 1], scale=1.0
+                )
+                nc.scalar.activation(
+                    out=dst[:, 0, :], in_=acc[:], func=SIGMOID, bias=neg_bias[:, row, col : col + 1], scale=-1.0
+                )
+
+            def to_batch_rows(src, first_bank, name):
+                turned = []
+                for pair in range(2):
+                    ps = bank(first_bank + pair, [P, 2, 2, P], "%s%d" % (name, pair))
+                    for a in range(2):
+                        bt = 2 * pair + a
+                        for side in range(2):
+                            nc.tensor.transpose(ps[:, a, side, :], src[:, side, bt * P : (bt + 1) * P], ident[:])
+                    turned.append(ps)
+                return turned
+
+            f_top = tree.tile([P, 2, BATCH], F32, name="f_top")
+            f_7 = tree.tile([P, 2, BATCH], F32, name="f_7")
+            branches(f_top, acc_top, 0, 0)
+            branches(f_7, acc_7, 0, 1)
+            late_run(0)
+            turned_top = to_batch_rows(f_top, 0, "turned_top")
+
+            f_8 = tree.tile([P, 2, 2, BATCH], F32, name="f_8")
+            for h in range(2):
+                branches(f_8[:, h], acc_8[h], 0, 2 + h)
+            late_run(1)
+            turned_7 = to_batch_rows(f_7, 2, "turned_7")
+
+            f_9 = tree.tile([P, 2, 2, 2, BATCH], F32, name="f_9")
+            for u in range(2):
+                branches(f_9[:, 0, u], acc_9[(0, u)], 1, 2 * u)
+
+            probs = tree.tile([P, BATCH_TILES, 1], F32, name="probs_0")
+            nc.vector.memset(probs[:], 1.0)
+            for level in range(8):
+                n = 2**level
+                turned, first = (turned_top, n - 1) if level < 7 else (turned_7, 0)
+                children = tree.tile([P, BATCH_TILES, 2 * n], F32, name="probs_%d" % (level + 1))
+                for pair in range(2):
+                    nc.vector.tensor_tensor(
+                        out=children[:, 2 * pair : 2 * pair + 2, :].rearrange("p a (j s) -> p a j s", s=2),
+                        in0=turned[pair][:, :, :, first : first + n].rearrange("p a s j -> p a j s"),
+                        in1=probs[:, 2 * pair : 2 * pair + 2, :].unsqueeze(3).to_broadcast([P, 2, n, 2]),
+                        op=MULT,
+                    )
+                probs = children
+
+            late_run(2)
+            probs_8 = [bank(4 + h, [P, BATCH], "probs_8_%d" % h) for h in range(2)]
+            for h in range(2):
+                for bt in range(BATCH_TILES):
+                    nc.tensor.transpose(
+                        probs_8[h][:, bt * P : (bt + 1) * P], probs[:, bt, h * P : (h + 1) * P], ident[:]
+                    )
+            late_run(3)
+
+            probs_9 = tree.tile([P, 2, 2, BATCH], F32, name="probs_9")
+            leaf_probs = tree.tile([P, 2, BATCH, 4], BF16, name="leaf_probs", align_bytes=64)
+            probs_codes = tree.tile([P, 2, BATCH], U32, name="probs_codes", align_bytes=64)
+            probs_scales = tree.tile([P, 2, BATCH], U8, name="probs_scales", align_bytes=64)
+            for h in range(2):
+                if h == 1:
+                    for u in range(2):
+                        branches(f_9[:, 1, u], acc_9[(1, u)], 1, 2 * u + 1)
+                nc.vector.tensor_tensor(
+                    out=probs_9[:, h],
+                    in0=probs_8[h][:].unsqueeze(1).to_broadcast([P, 2, BATCH]),
+                    in1=f_8[:, h],
+                    op=MULT,
+                )
+                nc.vector.tensor_tensor(
+                    out=leaf_probs[:, h].rearrange("p b (u e) -> p b u e", u=2),
+                    in0=probs_9[:, h].rearrange("p u b -> p b u").unsqueeze(3).to_broadcast([P, BATCH, 2, 2]),
+                    in1=f_9[:, h].rearrange("p u e b -> p b u e"),
+                    op=MULT,
+                )
+            for h in range(2):
+                nc.vector.quantize_mx(
+                    out=probs_codes[:, h, :].bitcast(FP8X4),
+                    scales=probs_scales[:, h, :],
+                    in_=leaf_probs[:, h].rearrange("p b t -> p (b t)"),
+                )
+
+            for bt in range(BATCH_TILES):
+                out_sb = result.tile([P, CLASSES], F32, name="out_sb")
+                for half_n in range(CLASSES // N_TILE):
+                    acc_out = bank(2 * (bt % 2) + half_n, [P, N_TILE], "acc_out")
+                    for h in range(2):
+                        nc.tensor.matmul_mx(
+                            out=acc_out[:],
+                            lhsT=probs_codes[:, h, bt * P : (bt + 1) * P].bitcast(FP8X4),
+                            lhsT_scale=probs_scales[:, h, bt * P : (bt + 1) * P],
+                            rhs=leaf_codes[:, h, 4 * N_TILE * half_n : 4 * N_TILE * (half_n + 1)].bitcast(FP8X4),
+                            rhs_scale=leaf_scales[:, h, N_TILE * half_n : N_TILE * (half_n + 1)],
+                            start=(h == 0),
+                            stop=(h == 1),
+                        )
+                    columns = out_sb[:, N_TILE * half_n : N_TILE * (half_n + 1)]
+                    if half_n == 0:
+                        nc.vector.tensor_copy(out=columns, in_=acc_out[:])
+                    else:
+                        nc.scalar.copy(out=columns, in_=acc_out[:])
+                nc.sync.dma_start(out=out[bt * P : (bt + 1) * P, :], in_=out_sb[:])

@@ -8,6 +8,7 @@ U32 = mybir.dt.uint32
 U8 = mybir.dt.uint8
 FP8X4 = mybir.dt.float8_e4m3fn_x4
 SIGMOID = mybir.ActivationFunctionType.Sigmoid
+COPY = mybir.ActivationFunctionType.Copy
 MULT = mybir.AluOpType.mult
 
 P = 128
@@ -16,6 +17,7 @@ FEATURES = 8192
 NODES = 1023
 CLASSES = 1024
 BATCH_TILES = BATCH // P
+HALF_BATCH = BATCH // 2
 K_PASS = 4 * P
 PASSES = FEATURES // K_PASS
 X_COLS = 2048
@@ -24,14 +26,17 @@ N_TILE = 512
 
 FIRST_7 = 127
 FIRST_9 = 511
-LATE_RUN = 8
+LATE_PASSES = 4 * PASSES
+LATE_RUN = 12
 
 FLOPS = 2 * BATCH * FEATURES * NODES + 2 * BATCH * CLASSES * CLASSES
 
 
 def tile_treemodel_k_kernel(tc, x, W_gate, b_gate, leaf_logits_words, leaf_logits_scales, out):
     nc = tc.nc
-    with tc.tile_pool(name="keep", bufs=1) as keep, tc.psum_pool(name="psum", bufs=1) as psum:
+    with tc.tile_pool(name="keep", bufs=1) as keep, tc.psum_pool(
+        name="psum", bufs=1
+    ) as psum, tc.manual_schedule():
 
         def bank(index, shape, name):
             return psum.tile(shape, F32, name=name, tag="bank%d" % index)
@@ -60,6 +65,10 @@ def tile_treemodel_k_kernel(tc, x, W_gate, b_gate, leaf_logits_words, leaf_logit
         nc.scalar.dma_start(
             out=rows_every_2nd[3:4, 0 : 2 * P - 1], in_=b_gate[FIRST_9 + 1 + 2 * P : NODES].unsqueeze(0)
         )
+        table_warm = keep.tile([P, 1], F32, name="table_warm")
+        nc.vector.memset(table_warm[:], 0.0)
+        nc.scalar.activation(out=table_warm[:], in_=table_warm[:], func=SIGMOID)
+
         rows_f32 = keep.tile([P, 2, P], F32, name="rows_f32")
         nc.vector.tensor_copy(out=rows_f32[:, 0, :], in_=rows_plain[:])
         nc.vector.tensor_copy(
@@ -69,27 +78,43 @@ def tile_treemodel_k_kernel(tc, x, W_gate, b_gate, leaf_logits_words, leaf_logit
         for i in range(2):
             nc.tensor.transpose(bias_ps[:, i, :], rows_f32[:, i, :], ident[:])
         bias = keep.tile([P, 2, 4], F32, name="bias")
-        neg_bias = keep.tile([P, 2, 4], F32, name="neg_bias")
         nc.vector.tensor_copy(out=bias[:], in_=bias_ps[:, :, 0:4])
-        nc.vector.tensor_scalar_mul(out=neg_bias[:], in0=bias[:], scalar1=-1.0)
+
+        def go_right(dst, logits, row, col):
+            nc.scalar.activation(
+                out=dst, in_=logits, func=SIGMOID, bias=bias[:, row, col : col + 1], scale=1.0
+            )
+
+        def go_left(dst, right):
+            nc.scalar.activation(out=dst, in_=right, func=COPY, bias=1.0, scale=-1.0)
+
+        def to_batch_rows(src, first_bank, name):
+            turned = []
+            for pair in range(2):
+                ps = bank(first_bank + pair, [P, 2, 2, P], "%s%d" % (name, pair))
+                for a in range(2):
+                    bt = 2 * pair + a
+                    for side in range(2):
+                        nc.tensor.transpose(ps[:, a, side, :], src[:, side, bt * P : (bt + 1) * P], ident[:])
+                turned.append(ps)
+            return turned
 
         x_codes = keep.tile([P, PASSES, BATCH], U32, name="x_codes", align_bytes=64)
         x_scales = keep.tile([P, PASSES, BATCH], U8, name="x_scales", align_bytes=64)
         late_codes = keep.tile([P, PASSES, 2 * P], U32, name="late_codes", align_bytes=64)
         late_scales = keep.tile([P, PASSES, 2 * P], U8, name="late_scales", align_bytes=64)
+        f_top = keep.tile([P, 2, BATCH], F32, name="f_top")
 
         acc_top = bank(0, [P, BATCH], "acc_top")
         acc_7 = bank(1, [P, BATCH], "acc_7")
         acc_8 = [bank(2 + h, [P, BATCH], "acc_8_%d" % h) for h in range(2)]
-        acc_9 = {(0, u): bank(4 + u, [P, BATCH], "acc_9_0_%d" % u) for u in range(2)}
+        acc_9 = [bank(4 + u, [P, BATCH], "acc_9_%d" % u) for u in range(2)]
 
-        streamed = [(acc_9[(0, 0)], 0), (acc_9[(0, 1)], P), (acc_7, 2 * P), (acc_8[0], 3 * P), (acc_8[1], 4 * P)]
+        streamed = [(acc_9[0], 0), (acc_9[1], P), (acc_7, 2 * P), (acc_8[0], 3 * P), (acc_8[1], 4 * P)]
 
         with tc.tile_pool(name="x_raw", bufs=2 * BATCH_TILES) as x_pool, tc.tile_pool(
             name="w_raw", bufs=4
-        ) as w_pool, tc.tile_pool(name="stage", bufs=2) as stage, tc.tile_pool(
-            name="codes", bufs=3
-        ) as codes_pool, tc.manual_schedule():
+        ) as w_pool, tc.tile_pool(name="stage", bufs=2) as stage, tc.tile_pool(name="codes", bufs=3) as codes_pool:
             x_raw = {}
             ready = {}
 
@@ -127,12 +152,14 @@ def tile_treemodel_k_kernel(tc, x, W_gate, b_gate, leaf_logits_words, leaf_logit
                 for h in range(2):
                     first = FIRST_9 + 2 * P * h
                     nc.vector.tensor_copy(
-                        out=w_grouped[:, 2 * P * h : 2 * P * (h + 1), :].rearrange("p (u m) t -> p u m t", u=2),
-                        in_=w_raw[:, :, first : first + 2 * P].rearrange("p t (m u) -> p u m t", u=2),
+                        out=w_grouped[:, 2 * P * h : 2 * P * (h + 1), :].rearrange(
+                            "p (u mo ml) t -> p mo t ml u", u=2, ml=2
+                        ),
+                        in_=w_raw[:, :, first : first + 2 * P].rearrange("p t (mo ml u) -> p mo t ml u", ml=2, u=2),
                     )
                 nc.scalar.copy(
-                    out=w_grouped[:, 4 * P : 7 * P, :],
-                    in_=w_raw[:, :, FIRST_7:FIRST_9].rearrange("p t n -> p n t"),
+                    out=w_grouped[:, 4 * P : 7 * P, :].rearrange("p (no i) t -> p no t i", i=4),
+                    in_=w_raw[:, :, FIRST_7:FIRST_9].rearrange("p t (no i) -> p no t i", i=4),
                 )
                 x_grouped = stage.tile([P, BATCH, 2], F32, name="x_grouped", align_bytes=64)
                 nc.vector.tensor_copy(out=x_grouped[:], in_=x_t[:].rearrange("p u b -> p b u"))
@@ -158,8 +185,8 @@ def tile_treemodel_k_kernel(tc, x, W_gate, b_gate, leaf_logits_words, leaf_logit
                 quantise_w(5 * P, 2 * P, w_codes[:, 3 * P : 5 * P], w_scales[:, 3 * P : 5 * P])
                 ready[c] = (w_raw, x_t, w_codes, w_scales)
 
-            def multiply(c):
-                w_raw, x_t, w_codes, w_scales = ready[c]
+            def multiply_plain(c):
+                w_raw, x_t = ready[c][0:2]
                 x_bf16 = x_t[:].bitcast(BF16).rearrange("p u (b e) -> p u b e", e=2)
                 for t in range(4):
                     nc.tensor.matmul(
@@ -169,6 +196,9 @@ def tile_treemodel_k_kernel(tc, x, W_gate, b_gate, leaf_logits_words, leaf_logit
                         start=(c == 0 and t == 0),
                         stop=(c == PASSES - 1 and t == 3),
                     )
+
+            def multiply_mx(c):
+                w_codes, w_scales = ready[c][2:4]
                 for acc, first in streamed:
                     nc.tensor.matmul_mx(
                         out=acc[:],
@@ -183,10 +213,16 @@ def tile_treemodel_k_kernel(tc, x, W_gate, b_gate, leaf_logits_words, leaf_logit
             for bt in range(BATCH_TILES):
                 load_x(0, bt)
             prepare(0)
+            multiply_plain(0)
             for c in range(1, PASSES):
                 prepare(c)
-                multiply(c - 1)
-            multiply(PASSES - 1)
+                multiply_mx(c - 1)
+                multiply_plain(c)
+
+            go_right(f_top[:, 1, :], acc_top[:], 0, 0)
+            go_left(f_top[:, 0, :], f_top[:, 1, :])
+            turned_top = to_batch_rows(f_top, 6, "turned_top")
+            multiply_mx(PASSES - 1)
 
             for q4 in range(4):
                 nc.sync.dma_start(
@@ -200,57 +236,37 @@ def tile_treemodel_k_kernel(tc, x, W_gate, b_gate, leaf_logits_words, leaf_logit
                 )
 
         with tc.tile_pool(name="tree", bufs=1) as tree, tc.tile_pool(name="result", bufs=2) as result:
-            for u in range(2):
-                acc_9[(1, u)] = bank(6 + u, [P, BATCH], "acc_9_1_%d" % u)
+            acc_late = []
 
-            def late_run(run):
-                for i in range(run * LATE_RUN, (run + 1) * LATE_RUN):
-                    u, c = divmod(i, PASSES)
+            def late_passes(first, count):
+                for i in range(first, first + count):
+                    half, u, c = i // (2 * PASSES), (i // PASSES) % 2, i % PASSES
+                    rows = slice(half * HALF_BATCH, (half + 1) * HALF_BATCH)
                     nc.tensor.matmul_mx(
-                        out=acc_9[(1, u)][:],
+                        out=acc_late[half][:, u, :],
                         lhsT=late_codes[:, c, u * P : (u + 1) * P].bitcast(FP8X4),
                         lhsT_scale=late_scales[:, c, u * P : (u + 1) * P],
-                        rhs=x_codes[:, c, :].bitcast(FP8X4),
-                        rhs_scale=x_scales[:, c, :],
+                        rhs=x_codes[:, c, rows].bitcast(FP8X4),
+                        rhs_scale=x_scales[:, c, rows],
                         start=(c == 0),
                         stop=(c == PASSES - 1),
                     )
 
-            def branches(dst, acc, row, col):
-                nc.scalar.activation(
-                    out=dst[:, 1, :], in_=acc[:], func=SIGMOID, bias=bias[:, row, col : col + 1], scale=1.0
-                )
-                nc.scalar.activation(
-                    out=dst[:, 0, :], in_=acc[:], func=SIGMOID, bias=neg_bias[:, row, col : col + 1], scale=-1.0
-                )
-
-            def to_batch_rows(src, first_bank, name):
-                turned = []
-                for pair in range(2):
-                    ps = bank(first_bank + pair, [P, 2, 2, P], "%s%d" % (name, pair))
-                    for a in range(2):
-                        bt = 2 * pair + a
-                        for side in range(2):
-                            nc.tensor.transpose(ps[:, a, side, :], src[:, side, bt * P : (bt + 1) * P], ident[:])
-                    turned.append(ps)
-                return turned
-
-            f_top = tree.tile([P, 2, BATCH], F32, name="f_top")
             f_7 = tree.tile([P, 2, BATCH], F32, name="f_7")
-            branches(f_top, acc_top, 0, 0)
-            branches(f_7, acc_7, 0, 1)
-            late_run(0)
-            turned_top = to_batch_rows(f_top, 0, "turned_top")
-
             f_8 = tree.tile([P, 2, 2, BATCH], F32, name="f_8")
-            for h in range(2):
-                branches(f_8[:, h], acc_8[h], 0, 2 + h)
-            late_run(1)
-            turned_7 = to_batch_rows(f_7, 2, "turned_7")
-
             f_9 = tree.tile([P, 2, 2, 2, BATCH], F32, name="f_9")
+            go_right(f_7[:, 1, :], acc_7[:], 0, 1)
+            go_left(f_7[:, 0, :], f_7[:, 1, :])
+            for h in range(2):
+                go_right(f_8[:, h, 1, :], acc_8[h][:], 0, 2 + h)
+            for half in range(2):
+                acc_late.append(bank(half, [P, 2, HALF_BATCH], "acc_late%d" % half))
+            late_passes(0, LATE_RUN)
+            turned_7 = to_batch_rows(f_7, 2, "turned_7")
+            go_left(f_8[:, :, 0, :], f_8[:, :, 1, :])
             for u in range(2):
-                branches(f_9[:, 0, u], acc_9[(0, u)], 1, 2 * u)
+                go_right(f_9[:, 0, u, 1, :], acc_9[u][:], 1, 2 * u)
+            go_left(f_9[:, 0, :, 0, :], f_9[:, 0, :, 1, :])
 
             probs = tree.tile([P, BATCH_TILES, 1], F32, name="probs_0")
             nc.vector.memset(probs[:], 1.0)
@@ -267,59 +283,68 @@ def tile_treemodel_k_kernel(tc, x, W_gate, b_gate, leaf_logits_words, leaf_logit
                     )
                 probs = children
 
-            late_run(2)
-            probs_8 = [bank(4 + h, [P, BATCH], "probs_8_%d" % h) for h in range(2)]
+            late_passes(LATE_RUN, LATE_RUN)
+            into_8 = [bank(6 + h, [P, BATCH], "into_8_%d" % h) for h in range(2)]
             for h in range(2):
                 for bt in range(BATCH_TILES):
                     nc.tensor.transpose(
-                        probs_8[h][:, bt * P : (bt + 1) * P], probs[:, bt, h * P : (h + 1) * P], ident[:]
+                        into_8[h][:, bt * P : (bt + 1) * P], probs[:, bt, h * P : (h + 1) * P], ident[:]
                     )
-            late_run(3)
+            late_passes(2 * LATE_RUN, LATE_PASSES - 2 * LATE_RUN)
 
-            probs_9 = tree.tile([P, 2, 2, BATCH], F32, name="probs_9")
+            into_9 = tree.tile([P, 2, 2, BATCH], F32, name="into_9")
             leaf_probs = tree.tile([P, 2, BATCH, 4], BF16, name="leaf_probs", align_bytes=64)
             probs_codes = tree.tile([P, 2, BATCH], U32, name="probs_codes", align_bytes=64)
             probs_scales = tree.tile([P, 2, BATCH], U8, name="probs_scales", align_bytes=64)
             for h in range(2):
-                if h == 1:
-                    for u in range(2):
-                        branches(f_9[:, 1, u], acc_9[(1, u)], 1, 2 * u + 1)
                 nc.vector.tensor_tensor(
-                    out=probs_9[:, h],
-                    in0=probs_8[h][:].unsqueeze(1).to_broadcast([P, 2, BATCH]),
+                    out=into_9[:, h],
+                    in0=into_8[h][:].unsqueeze(1).to_broadcast([P, 2, BATCH]),
                     in1=f_8[:, h],
                     op=MULT,
                 )
+
+            def leaves(h, first, count):
+                rows = slice(first, first + count)
                 nc.vector.tensor_tensor(
-                    out=leaf_probs[:, h].rearrange("p b (u e) -> p b u e", u=2),
-                    in0=probs_9[:, h].rearrange("p u b -> p b u").unsqueeze(3).to_broadcast([P, BATCH, 2, 2]),
-                    in1=f_9[:, h].rearrange("p u e b -> p b u e"),
+                    out=leaf_probs[:, h, rows, :].rearrange("p b (u e) -> p b u e", u=2),
+                    in0=into_9[:, h, :, rows].rearrange("p u b -> p b u").unsqueeze(3).to_broadcast([P, count, 2, 2]),
+                    in1=f_9[:, h, :, :, rows].rearrange("p u e b -> p b u e"),
                     op=MULT,
                 )
-            for h in range(2):
                 nc.vector.quantize_mx(
-                    out=probs_codes[:, h, :].bitcast(FP8X4),
-                    scales=probs_scales[:, h, :],
-                    in_=leaf_probs[:, h].rearrange("p b t -> p (b t)"),
+                    out=probs_codes[:, h, rows].bitcast(FP8X4),
+                    scales=probs_scales[:, h, rows],
+                    in_=leaf_probs[:, h, rows, :].rearrange("p b t -> p (b t)"),
                 )
 
-            for bt in range(BATCH_TILES):
-                out_sb = result.tile([P, CLASSES], F32, name="out_sb")
-                for half_n in range(CLASSES // N_TILE):
-                    acc_out = bank(2 * (bt % 2) + half_n, [P, N_TILE], "acc_out")
-                    for h in range(2):
-                        nc.tensor.matmul_mx(
-                            out=acc_out[:],
-                            lhsT=probs_codes[:, h, bt * P : (bt + 1) * P].bitcast(FP8X4),
-                            lhsT_scale=probs_scales[:, h, bt * P : (bt + 1) * P],
-                            rhs=leaf_codes[:, h, 4 * N_TILE * half_n : 4 * N_TILE * (half_n + 1)].bitcast(FP8X4),
-                            rhs_scale=leaf_scales[:, h, N_TILE * half_n : N_TILE * (half_n + 1)],
-                            start=(h == 0),
-                            stop=(h == 1),
-                        )
-                    columns = out_sb[:, N_TILE * half_n : N_TILE * (half_n + 1)]
-                    if half_n == 0:
-                        nc.vector.tensor_copy(out=columns, in_=acc_out[:])
-                    else:
-                        nc.scalar.copy(out=columns, in_=acc_out[:])
-                nc.sync.dma_start(out=out[bt * P : (bt + 1) * P, :], in_=out_sb[:])
+            leaves(0, 0, BATCH)
+
+            for half in range(2):
+                rows = slice(half * HALF_BATCH, (half + 1) * HALF_BATCH)
+                for u in range(2):
+                    go_right(f_9[:, 1, u, 1, rows], acc_late[half][:, u, :], 1, 2 * u + 1)
+                go_left(f_9[:, 1, :, 0, rows], f_9[:, 1, :, 1, rows])
+                leaves(1, half * HALF_BATCH, HALF_BATCH)
+
+            for half in range(2):
+                acc_out = {}
+                for h in range(2):
+                    for bt in range(2 * half, 2 * half + 2):
+                        for n in range(CLASSES // N_TILE):
+                            if h == 0:
+                                acc_out[(bt, n)] = bank((2 + 2 * bt + n) % 8, [P, N_TILE], "acc_out")
+                            nc.tensor.matmul_mx(
+                                out=acc_out[(bt, n)][:],
+                                lhsT=probs_codes[:, h, bt * P : (bt + 1) * P].bitcast(FP8X4),
+                                lhsT_scale=probs_scales[:, h, bt * P : (bt + 1) * P],
+                                rhs=leaf_codes[:, h, 4 * N_TILE * n : 4 * N_TILE * (n + 1)].bitcast(FP8X4),
+                                rhs_scale=leaf_scales[:, h, N_TILE * n : N_TILE * (n + 1)],
+                                start=(h == 0),
+                                stop=(h == 1),
+                            )
+                for bt in range(2 * half, 2 * half + 2):
+                    out_sb = result.tile([P, CLASSES], F32, name="out_sb")
+                    nc.vector.tensor_copy(out=out_sb[:, 0:N_TILE], in_=acc_out[(bt, 0)][:])
+                    nc.scalar.copy(out=out_sb[:, N_TILE:CLASSES], in_=acc_out[(bt, 1)][:])
+                    nc.sync.dma_start(out=out[bt * P : (bt + 1) * P, :], in_=out_sb[:])

@@ -20,7 +20,7 @@ BATCH_TILES = BATCH // P
 HALF_BATCH = BATCH // 2
 K_PASS = 4 * P
 PASSES = FEATURES // K_PASS
-X_COLS = 2048
+X_COLS = 1024
 PASSES_PER_X = X_COLS // K_PASS
 N_TILE = 512
 
@@ -112,112 +112,135 @@ def tile_treemodel_k_kernel(tc, x, W_gate, b_gate, leaf_logits_words, leaf_logit
 
         streamed = [(acc_9[0], 0), (acc_9[1], P), (acc_7, 2 * P), (acc_8[0], 3 * P), (acc_8[1], 4 * P)]
 
-        with tc.tile_pool(name="x_raw", bufs=2 * BATCH_TILES) as x_pool, tc.tile_pool(
+        with tc.tile_pool(name="x_raw", bufs=3 * BATCH_TILES) as x_pool, tc.tile_pool(
             name="w_raw", bufs=4
         ) as w_pool, tc.tile_pool(name="stage", bufs=2) as stage, tc.tile_pool(name="codes", bufs=3) as codes_pool:
             x_raw = {}
-            ready = {}
+            x_t = {}
+            x_grouped = {}
+            w_raw = {}
+            w_grouped = {}
+            w_codes = {}
+            w_scales = {}
 
-            def load_x(block, bt):
-                piece = x_pool.tile([P, X_COLS], BF16, name="x_piece")
-                nc.sync.dma_start(
-                    out=piece[:], in_=x[bt * P : (bt + 1) * P, block * X_COLS : (block + 1) * X_COLS]
-                )
-                x_raw[(block, bt)] = piece
+            def load_x(block):
+                for bt in range(BATCH_TILES):
+                    x_raw[(block, bt)] = x_pool.tile([P, X_COLS], BF16, name="x_piece")
+                    nc.sync.dma_start(
+                        out=x_raw[(block, bt)][:],
+                        in_=x[bt * P : (bt + 1) * P, block * X_COLS : (block + 1) * X_COLS],
+                    )
 
-            def prepare(c):
-                block, c_in_block = divmod(c, PASSES_PER_X)
-                w_raw = w_pool.tile([P, 4, NODES], BF16, name="w_raw")
+            def load_w(c):
+                w_raw[c] = w_pool.tile([P, 4, NODES], BF16, name="w_raw")
                 nc.sync.dma_start(
-                    out=w_raw[:].rearrange("p (u e) n -> p u e n", u=2),
+                    out=w_raw[c][:].rearrange("p (u e) n -> p u e n", u=2),
                     in_=W_gate[c * K_PASS : (c + 1) * K_PASS, :].rearrange("(u p e) n -> p u e n", u=2, p=P),
                 )
-                if block + 1 < FEATURES // X_COLS:
-                    load_x(block + 1, c_in_block)
 
-                xt_ps = [bank(6 + u, [P, BATCH], "xt_ps%d" % u) for u in range(2)]
+            def transpose_x(c):
+                block, c_in_block = divmod(c, PASSES_PER_X)
+                x_t[c] = stage.tile([P, 2, BATCH], F32, name="x_t")
                 for u in range(2):
+                    xt_ps = bank(6 + u, [P, BATCH], "xt_ps%d" % u)
+                    first = (2 * c_in_block + u) * P
                     for bt in range(BATCH_TILES):
-                        first = (2 * c_in_block + u) * P
                         nc.tensor.transpose(
-                            xt_ps[u][:, bt * P : (bt + 1) * P],
+                            xt_ps[:, bt * P : (bt + 1) * P],
                             x_raw[(block, bt)][:].bitcast(F32)[:, first : first + P],
                             ident[:],
                         )
-                x_t = stage.tile([P, 2, BATCH], F32, name="x_t")
-                for u in range(2):
-                    nc.scalar.copy(out=x_t[:, u, :], in_=xt_ps[u][:])
+                    nc.scalar.copy(out=x_t[c][:, u, :], in_=xt_ps[:])
 
-                w_grouped = stage.tile([P, 7 * P, 4], BF16, name="w_grouped", align_bytes=64)
-                for h in range(2):
-                    first = FIRST_9 + 2 * P * h
-                    nc.vector.tensor_copy(
-                        out=w_grouped[:, 2 * P * h : 2 * P * (h + 1), :].rearrange(
-                            "p (u mo ml) t -> p mo t ml u", u=2, ml=2
-                        ),
-                        in_=w_raw[:, :, first : first + 2 * P].rearrange("p t (mo ml u) -> p mo t ml u", ml=2, u=2),
-                    )
-                nc.scalar.copy(
-                    out=w_grouped[:, 4 * P : 7 * P, :].rearrange("p (no i) t -> p no t i", i=4),
-                    in_=w_raw[:, :, FIRST_7:FIRST_9].rearrange("p t (no i) -> p no t i", i=4),
-                )
-                x_grouped = stage.tile([P, BATCH, 2], F32, name="x_grouped", align_bytes=64)
-                nc.vector.tensor_copy(out=x_grouped[:], in_=x_t[:].rearrange("p u b -> p b u"))
+            def group_x(c):
+                x_grouped[c] = stage.tile([P, BATCH, 2], F32, name="x_grouped", align_bytes=64)
+                nc.vector.tensor_copy(out=x_grouped[c][:], in_=x_t[c][:].rearrange("p u b -> p b u"))
 
-                w_codes = codes_pool.tile([P, 5 * P], U32, name="w_codes", align_bytes=64)
-                w_scales = codes_pool.tile([P, 5 * P], U8, name="w_scales", align_bytes=64)
-
-                def quantise_w(first, count, codes, scales):
-                    nc.vector.quantize_mx(
-                        out=codes.bitcast(FP8X4),
-                        scales=scales,
-                        in_=w_grouped[:, first : first + count, :].rearrange("p n t -> p (n t)"),
-                    )
-
-                quantise_w(0, 2 * P, w_codes[:, 0 : 2 * P], w_scales[:, 0 : 2 * P])
-                quantise_w(2 * P, 2 * P, late_codes[:, c, :], late_scales[:, c, :])
+            def quantise_x(c):
                 nc.vector.quantize_mx(
                     out=x_codes[:, c, :].bitcast(FP8X4),
                     scales=x_scales[:, c, :],
-                    in_=x_grouped[:].rearrange("p b u -> p (b u)").bitcast(BF16),
+                    in_=x_grouped[c][:].rearrange("p b u -> p (b u)").bitcast(BF16),
                 )
-                quantise_w(4 * P, P, w_codes[:, 2 * P : 3 * P], w_scales[:, 2 * P : 3 * P])
-                quantise_w(5 * P, 2 * P, w_codes[:, 3 * P : 5 * P], w_scales[:, 3 * P : 5 * P])
-                ready[c] = (w_raw, x_t, w_codes, w_scales)
+
+            def group_w_level_9(c):
+                w_grouped[c] = stage.tile([P, 7 * P, 4], BF16, name="w_grouped", align_bytes=64)
+                for h in range(2):
+                    first = FIRST_9 + 2 * P * h
+                    nc.vector.tensor_copy(
+                        out=w_grouped[c][:, 2 * P * h : 2 * P * (h + 1), :].rearrange(
+                            "p (u mo ml) t -> p mo t ml u", u=2, ml=2
+                        ),
+                        in_=w_raw[c][:, :, first : first + 2 * P].rearrange(
+                            "p t (mo ml u) -> p mo t ml u", ml=2, u=2
+                        ),
+                    )
+
+            def group_w_levels_7_8(c):
+                nc.scalar.copy(
+                    out=w_grouped[c][:, 4 * P : 7 * P, :].rearrange("p (no i) t -> p no t i", i=4),
+                    in_=w_raw[c][:, :, FIRST_7:FIRST_9].rearrange("p t (no i) -> p no t i", i=4),
+                )
+
+            def quantise_w(c, first, count, codes, scales):
+                nc.vector.quantize_mx(
+                    out=codes.bitcast(FP8X4),
+                    scales=scales,
+                    in_=w_grouped[c][:, first : first + count, :].rearrange("p n t -> p (n t)"),
+                )
+
+            def quantise_w_level_9(c):
+                w_codes[c] = codes_pool.tile([P, 5 * P], U32, name="w_codes", align_bytes=64)
+                w_scales[c] = codes_pool.tile([P, 5 * P], U8, name="w_scales", align_bytes=64)
+                quantise_w(c, 0, 2 * P, w_codes[c][:, 0 : 2 * P], w_scales[c][:, 0 : 2 * P])
+                quantise_w(c, 2 * P, 2 * P, late_codes[:, c, :], late_scales[:, c, :])
+
+            def quantise_w_levels_7_8(c):
+                quantise_w(c, 4 * P, P, w_codes[c][:, 2 * P : 3 * P], w_scales[c][:, 2 * P : 3 * P])
+                quantise_w(c, 5 * P, 2 * P, w_codes[c][:, 3 * P : 5 * P], w_scales[c][:, 3 * P : 5 * P])
 
             def multiply_plain(c):
-                w_raw, x_t = ready[c][0:2]
-                x_bf16 = x_t[:].bitcast(BF16).rearrange("p u (b e) -> p u b e", e=2)
+                x_bf16 = x_t[c][:].bitcast(BF16).rearrange("p u (b e) -> p u b e", e=2)
                 for t in range(4):
                     nc.tensor.matmul(
                         out=acc_top[:],
-                        lhsT=w_raw[:, t, 0:P],
+                        lhsT=w_raw[c][:, t, 0:P],
                         rhs=x_bf16[:, t // 2, :, t % 2],
                         start=(c == 0 and t == 0),
                         stop=(c == PASSES - 1 and t == 3),
                     )
 
             def multiply_mx(c):
-                w_codes, w_scales = ready[c][2:4]
                 for acc, first in streamed:
                     nc.tensor.matmul_mx(
                         out=acc[:],
-                        lhsT=w_codes[:, first : first + P].bitcast(FP8X4),
-                        lhsT_scale=w_scales[:, first : first + P],
+                        lhsT=w_codes[c][:, first : first + P].bitcast(FP8X4),
+                        lhsT_scale=w_scales[c][:, first : first + P],
                         rhs=x_codes[:, c, :].bitcast(FP8X4),
                         rhs_scale=x_scales[:, c, :],
                         start=(c == 0),
                         stop=(c == PASSES - 1),
                     )
 
-            for bt in range(BATCH_TILES):
-                load_x(0, bt)
-            prepare(0)
-            multiply_plain(0)
-            for c in range(1, PASSES):
-                prepare(c)
-                multiply_mx(c - 1)
-                multiply_plain(c)
+            for s in range(-2, PASSES - 1):
+                if s + 2 < PASSES:
+                    if (s + 2) % PASSES_PER_X == 0:
+                        load_x((s + 2) // PASSES_PER_X)
+                    transpose_x(s + 2)
+                if s + 1 >= 0:
+                    load_w(s + 1)
+                    group_w_level_9(s + 1)
+                    group_w_levels_7_8(s + 1)
+                    quantise_x(s + 1)
+                    quantise_w_level_9(s + 1)
+                if s + 2 < PASSES:
+                    group_x(s + 2)
+                if s + 1 >= 0:
+                    quantise_w_levels_7_8(s + 1)
+                if s >= 0:
+                    multiply_mx(s)
+                if s + 1 >= 0:
+                    multiply_plain(s + 1)
 
             go_right(f_top[:, 1, :], acc_top[:], 0, 0)
             go_left(f_top[:, 0, :], f_top[:, 1, :])

@@ -69,16 +69,18 @@ def tile_treemodel_k_kernel(tc, x, W_gate, b_gate, leaf_logits_words, leaf_logit
         nc.vector.memset(table_warm[:], 0.0)
         nc.scalar.activation(out=table_warm[:], in_=table_warm[:], func=SIGMOID)
 
-        rows_f32 = keep.tile([P, 2, P], F32, name="rows_f32")
-        nc.vector.tensor_copy(out=rows_f32[:, 0, :], in_=rows_plain[:])
-        nc.vector.tensor_copy(
-            out=rows_f32[:, 1, :], in_=rows_every_2nd[:].rearrange("p (m two) -> p m two", two=2)[:, :, 0]
-        )
-        bias_ps = bank(6, [P, 2, P], "bias_ps")
-        for i in range(2):
-            nc.tensor.transpose(bias_ps[:, i, :], rows_f32[:, i, :], ident[:])
         bias = keep.tile([P, 2, 4], F32, name="bias")
-        nc.vector.tensor_copy(out=bias[:], in_=bias_ps[:, :, 0:4])
+
+        def bias_to_partitions():
+            rows_f32 = keep.tile([P, 2, P], F32, name="rows_f32")
+            nc.vector.tensor_copy(out=rows_f32[:, 0, :], in_=rows_plain[:])
+            nc.vector.tensor_copy(
+                out=rows_f32[:, 1, :], in_=rows_every_2nd[:].rearrange("p (m two) -> p m two", two=2)[:, :, 0]
+            )
+            bias_ps = bank(1, [P, 2, P], "bias_ps")
+            for i in range(2):
+                nc.tensor.transpose(bias_ps[:, i, :], rows_f32[:, i, :], ident[:])
+            nc.vector.tensor_copy(out=bias[:], in_=bias_ps[:, :, 0:4])
 
         def go_right(dst, logits, row, col):
             nc.scalar.activation(
@@ -106,11 +108,6 @@ def tile_treemodel_k_kernel(tc, x, W_gate, b_gate, leaf_logits_words, leaf_logit
         f_top = keep.tile([P, 2, BATCH], F32, name="f_top")
 
         acc_top = bank(0, [P, BATCH], "acc_top")
-        acc_7 = bank(1, [P, BATCH], "acc_7")
-        acc_8 = [bank(2 + h, [P, BATCH], "acc_8_%d" % h) for h in range(2)]
-        acc_9 = [bank(4 + u, [P, BATCH], "acc_9_%d" % u) for u in range(2)]
-
-        streamed = [(acc_9[0], 0), (acc_9[1], P), (acc_7, 2 * P), (acc_8[0], 3 * P), (acc_8[1], 4 * P)]
 
         with tc.tile_pool(name="x_raw", bufs=3 * BATCH_TILES) as x_pool, tc.tile_pool(
             name="w_raw", bufs=4
@@ -163,20 +160,22 @@ def tile_treemodel_k_kernel(tc, x, W_gate, b_gate, leaf_logits_words, leaf_logit
                     in_=x_grouped[c][:].rearrange("p b u -> p (b u)").bitcast(BF16),
                 )
 
-            def group_w_level_9(c):
-                w_grouped[c] = stage.tile([P, 7 * P, 4], BF16, name="w_grouped", align_bytes=64)
-                for h in range(2):
-                    first = FIRST_9 + 2 * P * h
-                    nc.vector.tensor_copy(
-                        out=w_grouped[c][:, 2 * P * h : 2 * P * (h + 1), :].rearrange(
-                            "p (u mo ml) t -> p mo t ml u", u=2, ml=2
-                        ),
-                        in_=w_raw[c][:, :, first : first + 2 * P].rearrange(
-                            "p t (mo ml u) -> p mo t ml u", ml=2, u=2
-                        ),
-                    )
+            def every_2nd_node(c, h):
+                first = FIRST_9 + 2 * P * h
+                return (
+                    w_raw[c][:, :, first : first + 2 * P].rearrange("p t (mo i u) -> p u mo t i", i=4, u=2),
+                    w_grouped[c][:, 2 * P * h : 2 * P * (h + 1), :].rearrange("p (u mo i) t -> p u mo t i", u=2, i=4),
+                )
 
-            def group_w_levels_7_8(c):
+            def group_w_on_vector(c):
+                w_grouped[c] = stage.tile([P, 7 * P, 4], BF16, name="w_grouped", align_bytes=64)
+                for h, u in ((0, 0), (0, 1), (1, 0)):
+                    src, dst = every_2nd_node(c, h)
+                    nc.vector.tensor_copy(out=dst[:, u], in_=src[:, u])
+
+            def group_w_on_scalar(c):
+                src, dst = every_2nd_node(c, 1)
+                nc.scalar.copy(out=dst[:, 1], in_=src[:, 1])
                 nc.scalar.copy(
                     out=w_grouped[c][:, 4 * P : 7 * P, :].rearrange("p (no i) t -> p no t i", i=4),
                     in_=w_raw[c][:, :, FIRST_7:FIRST_9].rearrange("p t (no i) -> p no t i", i=4),
@@ -189,13 +188,13 @@ def tile_treemodel_k_kernel(tc, x, W_gate, b_gate, leaf_logits_words, leaf_logit
                     in_=w_grouped[c][:, first : first + count, :].rearrange("p n t -> p (n t)"),
                 )
 
-            def quantise_w_level_9(c):
+            def quantise_w_from_vector(c):
                 w_codes[c] = codes_pool.tile([P, 5 * P], U32, name="w_codes", align_bytes=64)
                 w_scales[c] = codes_pool.tile([P, 5 * P], U8, name="w_scales", align_bytes=64)
                 quantise_w(c, 0, 2 * P, w_codes[c][:, 0 : 2 * P], w_scales[c][:, 0 : 2 * P])
-                quantise_w(c, 2 * P, 2 * P, late_codes[:, c, :], late_scales[:, c, :])
 
-            def quantise_w_levels_7_8(c):
+            def quantise_w_from_scalar(c):
+                quantise_w(c, 2 * P, 2 * P, late_codes[:, c, :], late_scales[:, c, :])
                 quantise_w(c, 4 * P, P, w_codes[c][:, 2 * P : 3 * P], w_scales[c][:, 2 * P : 3 * P])
                 quantise_w(c, 5 * P, 2 * P, w_codes[c][:, 3 * P : 5 * P], w_scales[c][:, 3 * P : 5 * P])
 
@@ -222,25 +221,35 @@ def tile_treemodel_k_kernel(tc, x, W_gate, b_gate, leaf_logits_words, leaf_logit
                         stop=(c == PASSES - 1),
                     )
 
-            for s in range(-2, PASSES - 1):
+            def step(s):
                 if s + 2 < PASSES:
                     if (s + 2) % PASSES_PER_X == 0:
                         load_x((s + 2) // PASSES_PER_X)
                     transpose_x(s + 2)
                 if s + 1 >= 0:
                     load_w(s + 1)
-                    group_w_level_9(s + 1)
-                    group_w_levels_7_8(s + 1)
+                    group_w_on_vector(s + 1)
+                    group_w_on_scalar(s + 1)
                     quantise_x(s + 1)
-                    quantise_w_level_9(s + 1)
+                    quantise_w_from_vector(s + 1)
                 if s + 2 < PASSES:
                     group_x(s + 2)
                 if s + 1 >= 0:
-                    quantise_w_levels_7_8(s + 1)
+                    quantise_w_from_scalar(s + 1)
                 if s >= 0:
                     multiply_mx(s)
                 if s + 1 >= 0:
                     multiply_plain(s + 1)
+
+            step(-2)
+            step(-1)
+            bias_to_partitions()
+            acc_7 = bank(1, [P, BATCH], "acc_7")
+            acc_8 = [bank(2 + h, [P, BATCH], "acc_8_%d" % h) for h in range(2)]
+            acc_9 = [bank(4 + u, [P, BATCH], "acc_9_%d" % u) for u in range(2)]
+            streamed = [(acc_9[0], 0), (acc_9[1], P), (acc_7, 2 * P), (acc_8[0], 3 * P), (acc_8[1], 4 * P)]
+            for s in range(PASSES - 1):
+                step(s)
 
             go_right(f_top[:, 1, :], acc_top[:], 0, 0)
             go_left(f_top[:, 0, :], f_top[:, 1, :])

@@ -247,14 +247,14 @@ def tile_treemodel_k_kernel(tc, x, W_gate, b_gate, leaf_logits_words, leaf_logit
             acc_7 = bank(1, [P, BATCH], "acc_7")
             acc_8 = [bank(2 + h, [P, BATCH], "acc_8_%d" % h) for h in range(2)]
             acc_9 = [bank(4 + u, [P, BATCH], "acc_9_%d" % u) for u in range(2)]
-            streamed = [(acc_9[0], 0), (acc_9[1], P), (acc_7, 2 * P), (acc_8[0], 3 * P), (acc_8[1], 4 * P)]
+            streamed = [(acc_7, 2 * P), (acc_8[0], 3 * P), (acc_8[1], 4 * P), (acc_9[0], 0), (acc_9[1], P)]
             for s in range(PASSES - 1):
                 step(s)
 
             go_right(f_top[:, 1, :], acc_top[:], 0, 0)
             go_left(f_top[:, 0, :], f_top[:, 1, :])
-            turned_top = to_batch_rows(f_top, 6, "turned_top")
             multiply_mx(PASSES - 1)
+            turned_top = to_batch_rows(f_top, 6, "turned_top")
 
             for q4 in range(4):
                 nc.sync.dma_start(
@@ -267,7 +267,7 @@ def tile_treemodel_k_kernel(tc, x, W_gate, b_gate, leaf_logits_words, leaf_logit
                     in_=leaf_logits_words[h].rearrange("p n t -> p (n t)").bitcast(I32),
                 )
 
-        with tc.tile_pool(name="tree", bufs=1) as tree, tc.tile_pool(name="result", bufs=2) as result:
+        with tc.tile_pool(name="tree", bufs=1) as tree, tc.tile_pool(name="result", bufs=BATCH_TILES) as result:
             acc_late = []
 
             def late_passes(first, count):

@@ -28,6 +28,7 @@ FIRST_7 = 127
 FIRST_9 = 511
 LATE_PASSES = 4 * PASSES
 LATE_RUN = 12
+SHARED_CUT = 16
 
 FLOPS = 2 * BATCH * FEATURES * NODES + 2 * BATCH * CLASSES * CLASSES
 
@@ -106,6 +107,7 @@ def tile_treemodel_k_kernel(tc, x, W_gate, b_gate, leaf_logits_words, leaf_logit
         late_codes = keep.tile([P, PASSES, 2 * P], U32, name="late_codes", align_bytes=64)
         late_scales = keep.tile([P, PASSES, 2 * P], U8, name="late_scales", align_bytes=64)
         f_top = keep.tile([P, 2, BATCH], F32, name="f_top")
+        f_7 = keep.tile([P, 2, BATCH], F32, name="f_7")
 
         acc_top = bank(0, [P, BATCH], "acc_top")
 
@@ -172,10 +174,12 @@ def tile_treemodel_k_kernel(tc, x, W_gate, b_gate, leaf_logits_words, leaf_logit
                 for h, u in ((0, 0), (0, 1), (1, 0)):
                     src, dst = every_2nd_node(c, h)
                     nc.vector.tensor_copy(out=dst[:, u], in_=src[:, u])
+                src, dst = every_2nd_node(c, 1)
+                nc.vector.tensor_copy(out=dst[:, 1, 0:SHARED_CUT], in_=src[:, 1, 0:SHARED_CUT])
 
             def group_w_on_scalar(c):
                 src, dst = every_2nd_node(c, 1)
-                nc.scalar.copy(out=dst[:, 1], in_=src[:, 1])
+                nc.scalar.copy(out=dst[:, 1, SHARED_CUT:], in_=src[:, 1, SHARED_CUT:])
                 nc.scalar.copy(
                     out=w_grouped[c][:, 4 * P : 7 * P, :].rearrange("p (no i) t -> p no t i", i=4),
                     in_=w_raw[c][:, :, FIRST_7:FIRST_9].rearrange("p t (no i) -> p no t i", i=4),
@@ -209,8 +213,8 @@ def tile_treemodel_k_kernel(tc, x, W_gate, b_gate, leaf_logits_words, leaf_logit
                         stop=(c == PASSES - 1 and t == 3),
                     )
 
-            def multiply_mx(c):
-                for acc, first in streamed:
+            def multiply_mx(c, tiles):
+                for acc, first in tiles:
                     nc.tensor.matmul_mx(
                         out=acc[:],
                         lhsT=w_codes[c][:, first : first + P].bitcast(FP8X4),
@@ -237,7 +241,7 @@ def tile_treemodel_k_kernel(tc, x, W_gate, b_gate, leaf_logits_words, leaf_logit
                 if s + 1 >= 0:
                     quantise_w_from_scalar(s + 1)
                 if s >= 0:
-                    multiply_mx(s)
+                    multiply_mx(s, streamed)
                 if s + 1 >= 0:
                     multiply_plain(s + 1)
 
@@ -248,13 +252,38 @@ def tile_treemodel_k_kernel(tc, x, W_gate, b_gate, leaf_logits_words, leaf_logit
             acc_8 = [bank(2 + h, [P, BATCH], "acc_8_%d" % h) for h in range(2)]
             acc_9 = [bank(4 + u, [P, BATCH], "acc_9_%d" % u) for u in range(2)]
             streamed = [(acc_7, 2 * P), (acc_8[0], 3 * P), (acc_8[1], 4 * P), (acc_9[0], 0), (acc_9[1], P)]
-            for s in range(PASSES - 1):
+            for s in range(PASSES - 2):
                 step(s)
 
+            last = PASSES - 1
+            load_w(last)
+            w_grouped[last] = stage.tile([P, 7 * P, 4], BF16, name="w_grouped", align_bytes=64)
+            w_codes[last] = codes_pool.tile([P, 5 * P], U32, name="w_codes", align_bytes=64)
+            w_scales[last] = codes_pool.tile([P, 5 * P], U8, name="w_scales", align_bytes=64)
+            nc.vector.tensor_copy(
+                out=w_grouped[last][:, 4 * P : 7 * P, :].rearrange("p (no i) t -> p no t i", i=4),
+                in_=w_raw[last][:, :, FIRST_7:FIRST_9].rearrange("p t (no i) -> p no t i", i=4),
+            )
+            quantise_x(last)
+            quantise_w(last, 4 * P, P, w_codes[last][:, 2 * P : 3 * P], w_scales[last][:, 2 * P : 3 * P])
+            quantise_w(last, 5 * P, 2 * P, w_codes[last][:, 3 * P : 5 * P], w_scales[last][:, 3 * P : 5 * P])
+            src, dst = every_2nd_node(last, 0)
+            for u in range(2):
+                nc.scalar.copy(out=dst[:, u], in_=src[:, u])
+            multiply_plain(last)
+            multiply_mx(last - 1, streamed)
             go_right(f_top[:, 1, :], acc_top[:], 0, 0)
             go_left(f_top[:, 0, :], f_top[:, 1, :])
-            multiply_mx(PASSES - 1)
+            multiply_mx(last, streamed[0:3])
+            quantise_w(last, 0, 2 * P, w_codes[last][:, 0 : 2 * P], w_scales[last][:, 0 : 2 * P])
             turned_top = to_batch_rows(f_top, 6, "turned_top")
+            multiply_mx(last, streamed[3:5])
+            src, dst = every_2nd_node(last, 1)
+            nc.scalar.copy(out=dst[:, 0], in_=src[:, 0])
+            go_right(f_7[:, 1, :], acc_7[:], 0, 1)
+            go_left(f_7[:, 0, :], f_7[:, 1, :])
+            nc.scalar.copy(out=dst[:, 1], in_=src[:, 1])
+            quantise_w(last, 2 * P, 2 * P, late_codes[:, last, :], late_scales[:, last, :])
 
             for q4 in range(4):
                 nc.sync.dma_start(
@@ -284,11 +313,8 @@ def tile_treemodel_k_kernel(tc, x, W_gate, b_gate, leaf_logits_words, leaf_logit
                         stop=(c == PASSES - 1),
                     )
 
-            f_7 = tree.tile([P, 2, BATCH], F32, name="f_7")
             f_8 = tree.tile([P, 2, 2, BATCH], F32, name="f_8")
             f_9 = tree.tile([P, 2, 2, 2, BATCH], F32, name="f_9")
-            go_right(f_7[:, 1, :], acc_7[:], 0, 1)
-            go_left(f_7[:, 0, :], f_7[:, 1, :])
             for h in range(2):
                 go_right(f_8[:, h, 1, :], acc_8[h][:], 0, 2 + h)
             for half in range(2):
@@ -378,5 +404,6 @@ def tile_treemodel_k_kernel(tc, x, W_gate, b_gate, leaf_logits_words, leaf_logit
                 for bt in range(2 * half, 2 * half + 2):
                     out_sb = result.tile([P, CLASSES], F32, name="out_sb")
                     nc.vector.tensor_copy(out=out_sb[:, 0:N_TILE], in_=acc_out[(bt, 0)][:])
+                    nc.sync.dma_start(out=out[bt * P : (bt + 1) * P, 0:N_TILE], in_=out_sb[:, 0:N_TILE])
                     nc.scalar.copy(out=out_sb[:, N_TILE:CLASSES], in_=acc_out[(bt, 1)][:])
-                    nc.sync.dma_start(out=out[bt * P : (bt + 1) * P, :], in_=out_sb[:])
+                    nc.scalar.dma_start(out=out[bt * P : (bt + 1) * P, N_TILE:CLASSES], in_=out_sb[:, N_TILE:CLASSES])

@@ -23,6 +23,7 @@ PASSES = FEATURES // K_PASS
 X_COLS = 1024
 PASSES_PER_X = X_COLS // K_PASS
 N_TILE = 512
+W_RUN_PITCH = 2048
 
 FIRST_7 = 127
 FIRST_9 = 511
@@ -131,9 +132,10 @@ def tile_treemodel_k_kernel(tc, x, W_gate, b_gate, leaf_logits_words, leaf_logit
                     )
 
             def load_w(c):
-                w_raw[c] = w_pool.tile([P, 4, NODES], BF16, name="w_raw")
+                w_tile = w_pool.tile([P, 2, W_RUN_PITCH], BF16, name="w_raw")
+                w_raw[c] = w_tile[:, :, 0 : 2 * NODES].rearrange("p u (e n) -> p u e n", e=2)
                 nc.sync.dma_start(
-                    out=w_raw[c][:].rearrange("p (u e) n -> p u e n", u=2),
+                    out=w_raw[c],
                     in_=W_gate[c * K_PASS : (c + 1) * K_PASS, :].rearrange("(u p e) n -> p u e n", u=2, p=P),
                 )
 
@@ -165,8 +167,10 @@ def tile_treemodel_k_kernel(tc, x, W_gate, b_gate, leaf_logits_words, leaf_logit
             def every_2nd_node(c, h):
                 first = FIRST_9 + 2 * P * h
                 return (
-                    w_raw[c][:, :, first : first + 2 * P].rearrange("p t (mo i u) -> p u mo t i", i=4, u=2),
-                    w_grouped[c][:, 2 * P * h : 2 * P * (h + 1), :].rearrange("p (u mo i) t -> p u mo t i", u=2, i=4),
+                    w_raw[c][:, :, :, first : first + 2 * P].rearrange("p a e (mo i u) -> p u mo a e i", i=4, u=2),
+                    w_grouped[c][:, 2 * P * h : 2 * P * (h + 1), :].rearrange(
+                        "p (u mo i) (a e) -> p u mo a e i", u=2, i=4, a=2
+                    ),
                 )
 
             def group_w_on_vector(c):
@@ -181,8 +185,8 @@ def tile_treemodel_k_kernel(tc, x, W_gate, b_gate, leaf_logits_words, leaf_logit
                 src, dst = every_2nd_node(c, 1)
                 nc.scalar.copy(out=dst[:, 1, SHARED_CUT:], in_=src[:, 1, SHARED_CUT:])
                 nc.scalar.copy(
-                    out=w_grouped[c][:, 4 * P : 7 * P, :].rearrange("p (no i) t -> p no t i", i=4),
-                    in_=w_raw[c][:, :, FIRST_7:FIRST_9].rearrange("p t (no i) -> p no t i", i=4),
+                    out=w_grouped[c][:, 4 * P : 7 * P, :].rearrange("p (no i) (a e) -> p no a e i", i=4, a=2),
+                    in_=w_raw[c][:, :, :, FIRST_7:FIRST_9].rearrange("p a e (no i) -> p no a e i", i=4),
                 )
 
             def quantise_w(c, first, count, codes, scales):
@@ -207,7 +211,7 @@ def tile_treemodel_k_kernel(tc, x, W_gate, b_gate, leaf_logits_words, leaf_logit
                 for t in range(4):
                     nc.tensor.matmul(
                         out=acc_top[:],
-                        lhsT=w_raw[c][:, t, 0:P],
+                        lhsT=w_raw[c][:, t // 2, t % 2, 0:P],
                         rhs=x_bf16[:, t // 2, :, t % 2],
                         start=(c == 0 and t == 0),
                         stop=(c == PASSES - 1 and t == 3),
@@ -261,8 +265,8 @@ def tile_treemodel_k_kernel(tc, x, W_gate, b_gate, leaf_logits_words, leaf_logit
             w_codes[last] = codes_pool.tile([P, 5 * P], U32, name="w_codes", align_bytes=64)
             w_scales[last] = codes_pool.tile([P, 5 * P], U8, name="w_scales", align_bytes=64)
             nc.vector.tensor_copy(
-                out=w_grouped[last][:, 4 * P : 7 * P, :].rearrange("p (no i) t -> p no t i", i=4),
-                in_=w_raw[last][:, :, FIRST_7:FIRST_9].rearrange("p t (no i) -> p no t i", i=4),
+                out=w_grouped[last][:, 4 * P : 7 * P, :].rearrange("p (no i) (a e) -> p no a e i", i=4, a=2),
+                in_=w_raw[last][:, :, :, FIRST_7:FIRST_9].rearrange("p a e (no i) -> p no a e i", i=4),
             )
             quantise_x(last)
             quantise_w(last, 4 * P, P, w_codes[last][:, 2 * P : 3 * P], w_scales[last][:, 2 * P : 3 * P])

@@ -29,6 +29,7 @@ FIRST_7 = 127
 FIRST_9 = 511
 LATE_PASSES = 4 * PASSES
 LATE_RUN = 12
+OUT_BANKS = (0, 1, 4, 5, 6, 7, 2, 3)
 SHARED_CUT = 16
 
 FLOPS = 2 * BATCH * FEATURES * NODES + 2 * BATCH * CLASSES * CLASSES
@@ -319,12 +320,12 @@ def tile_treemodel_k_kernel(tc, x, W_gate, b_gate, leaf_logits_words, leaf_logit
 
             f_8 = tree.tile([P, 2, 2, BATCH], F32, name="f_8")
             f_9 = tree.tile([P, 2, 2, 2, BATCH], F32, name="f_9")
+            turned_7 = to_batch_rows(f_7, 0, "turned_7")
             for h in range(2):
                 go_right(f_8[:, h, 1, :], acc_8[h][:], 0, 2 + h)
             for half in range(2):
-                acc_late.append(bank(half, [P, 2, HALF_BATCH], "acc_late%d" % half))
+                acc_late.append(bank(2 + half, [P, 2, HALF_BATCH], "acc_late%d" % half))
             late_passes(0, LATE_RUN)
-            turned_7 = to_batch_rows(f_7, 2, "turned_7")
             go_left(f_8[:, :, 0, :], f_8[:, :, 1, :])
             for u in range(2):
                 go_right(f_9[:, 0, u, 1, :], acc_9[u][:], 1, 2 * u)
@@ -386,7 +387,7 @@ def tile_treemodel_k_kernel(tc, x, W_gate, b_gate, leaf_logits_words, leaf_logit
                 rows = slice(half * HALF_BATCH, (half + 1) * HALF_BATCH)
                 for u in range(2):
                     go_right(f_9[:, 1, u, 1, rows], acc_late[half][:, u, :], 1, 2 * u + 1)
-                go_left(f_9[:, 1, :, 0, rows], f_9[:, 1, :, 1, rows])
+                    go_left(f_9[:, 1, u, 0, rows], f_9[:, 1, u, 1, rows])
                 leaves(1, half * HALF_BATCH, HALF_BATCH)
 
             for half in range(2):
@@ -395,7 +396,7 @@ def tile_treemodel_k_kernel(tc, x, W_gate, b_gate, leaf_logits_words, leaf_logit
                     for bt in range(2 * half, 2 * half + 2):
                         for n in range(CLASSES // N_TILE):
                             if h == 0:
-                                acc_out[(bt, n)] = bank((2 + 2 * bt + n) % 8, [P, N_TILE], "acc_out")
+                                acc_out[(bt, n)] = bank(OUT_BANKS[2 * bt + n], [P, N_TILE], "acc_out")
                             nc.tensor.matmul_mx(
                                 out=acc_out[(bt, n)][:],
                                 lhsT=probs_codes[:, h, bt * P : (bt + 1) * P].bitcast(FP8X4),

@@ -331,64 +331,83 @@ def tile_treemodel_k_kernel(tc, x, W_gate, b_gate, leaf_logits_words, leaf_logit
                 go_right(f_9[:, 0, u, 1, :], acc_9[u][:], 1, 2 * u)
             go_left(f_9[:, 0, :, 0, :], f_9[:, 0, :, 1, :])
 
-            probs = tree.tile([P, BATCH_TILES, 1], F32, name="probs_0")
-            nc.vector.memset(probs[:], 1.0)
+            probs = []
+            for pair in range(2):
+                root = tree.tile([P, 2, 1], F32, name="probs_0_%d" % pair)
+                nc.vector.memset(root[:], 1.0)
+                probs.append(root)
             for level in range(8):
                 n = 2**level
                 turned, first = (turned_top, n - 1) if level < 7 else (turned_7, 0)
-                children = tree.tile([P, BATCH_TILES, 2 * n], F32, name="probs_%d" % (level + 1))
                 for pair in range(2):
+                    children = tree.tile([P, 2, 2 * n], F32, name="probs_%d_%d" % (level + 1, pair))
                     nc.vector.tensor_tensor(
-                        out=children[:, 2 * pair : 2 * pair + 2, :].rearrange("p a (j s) -> p a j s", s=2),
+                        out=children[:].rearrange("p a (j s) -> p a j s", s=2),
                         in0=turned[pair][:, :, :, first : first + n].rearrange("p a s j -> p a j s"),
-                        in1=probs[:, 2 * pair : 2 * pair + 2, :].unsqueeze(3).to_broadcast([P, 2, n, 2]),
+                        in1=probs[pair][:].unsqueeze(3).to_broadcast([P, 2, n, 2]),
                         op=MULT,
                     )
-                probs = children
+                    probs[pair] = children
 
             late_passes(LATE_RUN, LATE_RUN)
-            into_8 = [bank(6 + h, [P, BATCH], "into_8_%d" % h) for h in range(2)]
-            for h in range(2):
-                for bt in range(BATCH_TILES):
-                    nc.tensor.transpose(
-                        into_8[h][:, bt * P : (bt + 1) * P], probs[:, bt, h * P : (h + 1) * P], ident[:]
-                    )
+            into_8 = []
+            for half in range(2):
+                into_8.append(bank(6 + half, [P, 2, HALF_BATCH], "into_8_%d" % half))
+                for h in range(2):
+                    for a in range(2):
+                        nc.tensor.transpose(
+                            into_8[half][:, h, a * P : (a + 1) * P], probs[half][:, a, h * P : (h + 1) * P], ident[:]
+                        )
             late_passes(2 * LATE_RUN, LATE_PASSES - 2 * LATE_RUN)
 
             into_9 = tree.tile([P, 2, 2, BATCH], F32, name="into_9")
             leaf_probs = tree.tile([P, 2, BATCH, 4], BF16, name="leaf_probs", align_bytes=64)
             probs_codes = tree.tile([P, 2, BATCH], U32, name="probs_codes", align_bytes=64)
             probs_scales = tree.tile([P, 2, BATCH], U8, name="probs_scales", align_bytes=64)
-            for h in range(2):
+            half_rows = [slice(half * HALF_BATCH, (half + 1) * HALF_BATCH) for half in range(2)]
+            for half in range(2):
                 nc.vector.tensor_tensor(
-                    out=into_9[:, h],
-                    in0=into_8[h][:].unsqueeze(1).to_broadcast([P, 2, BATCH]),
-                    in1=f_8[:, h],
+                    out=into_9[:, :, :, half_rows[half]],
+                    in0=into_8[half][:].unsqueeze(2).to_broadcast([P, 2, 2, HALF_BATCH]),
+                    in1=f_8[:, :, :, half_rows[half]],
                     op=MULT,
                 )
 
-            def leaves(h, first, count):
-                rows = slice(first, first + count)
+            def multiply_leaves(h, half):
+                rows = half_rows[half]
                 nc.vector.tensor_tensor(
                     out=leaf_probs[:, h, rows, :].rearrange("p b (u e) -> p b u e", u=2),
-                    in0=into_9[:, h, :, rows].rearrange("p u b -> p b u").unsqueeze(3).to_broadcast([P, count, 2, 2]),
+                    in0=into_9[:, h, :, rows]
+                    .rearrange("p u b -> p b u")
+                    .unsqueeze(3)
+                    .to_broadcast([P, HALF_BATCH, 2, 2]),
                     in1=f_9[:, h, :, :, rows].rearrange("p u e b -> p b u e"),
                     op=MULT,
                 )
+
+            def quantise_leaves(h, half):
+                rows = half_rows[half]
                 nc.vector.quantize_mx(
                     out=probs_codes[:, h, rows].bitcast(FP8X4),
                     scales=probs_scales[:, h, rows],
                     in_=leaf_probs[:, h, rows, :].rearrange("p b t -> p (b t)"),
                 )
 
-            leaves(0, 0, BATCH)
-
-            for half in range(2):
-                rows = slice(half * HALF_BATCH, (half + 1) * HALF_BATCH)
+            def late_branches(half):
                 for u in range(2):
-                    go_right(f_9[:, 1, u, 1, rows], acc_late[half][:, u, :], 1, 2 * u + 1)
-                    go_left(f_9[:, 1, u, 0, rows], f_9[:, 1, u, 1, rows])
-                leaves(1, half * HALF_BATCH, HALF_BATCH)
+                    go_right(f_9[:, 1, u, 1, half_rows[half]], acc_late[half][:, u, :], 1, 2 * u + 1)
+                    go_left(f_9[:, 1, u, 0, half_rows[half]], f_9[:, 1, u, 1, half_rows[half]])
+
+            multiply_leaves(0, 0)
+            multiply_leaves(0, 1)
+            quantise_leaves(0, 0)
+            late_branches(0)
+            multiply_leaves(1, 0)
+            quantise_leaves(0, 1)
+            quantise_leaves(1, 0)
+            late_branches(1)
+            multiply_leaves(1, 1)
+            quantise_leaves(1, 1)
 
             for half in range(2):
                 acc_out = {}

@@ -276,12 +276,13 @@ def tile_treemodel_k_kernel(tc, x, W_gate, b_gate, leaf_logits_words, leaf_logit
             for u in range(2):
                 nc.scalar.copy(out=dst[:, u], in_=src[:, u])
             multiply_plain(last)
-            multiply_mx(last - 1, streamed)
+            multiply_mx(last - 1, streamed[0:3])
             go_right(f_top[:, 1, :], acc_top[:], 0, 0)
             go_left(f_top[:, 0, :], f_top[:, 1, :])
             multiply_mx(last, streamed[0:3])
             quantise_w(last, 0, 2 * P, w_codes[last][:, 0 : 2 * P], w_scales[last][:, 0 : 2 * P])
             turned_top = to_batch_rows(f_top, 6, "turned_top")
+            multiply_mx(last - 1, streamed[3:5])
             multiply_mx(last, streamed[3:5])
             src, dst = every_2nd_node(last, 1)
             nc.scalar.copy(out=dst[:, 0], in_=src[:, 0])
@@ -373,20 +374,18 @@ def tile_treemodel_k_kernel(tc, x, W_gate, b_gate, leaf_logits_words, leaf_logit
                     op=MULT,
                 )
 
-            def multiply_leaves(h, half):
-                rows = half_rows[half]
+            def multiply_leaves(h, rows):
                 nc.vector.tensor_tensor(
                     out=leaf_probs[:, h, rows, :].rearrange("p b (u e) -> p b u e", u=2),
                     in0=into_9[:, h, :, rows]
                     .rearrange("p u b -> p b u")
                     .unsqueeze(3)
-                    .to_broadcast([P, HALF_BATCH, 2, 2]),
+                    .to_broadcast([P, rows.stop - rows.start, 2, 2]),
                     in1=f_9[:, h, :, :, rows].rearrange("p u e b -> p b u e"),
                     op=MULT,
                 )
 
-            def quantise_leaves(h, half):
-                rows = half_rows[half]
+            def quantise_leaves(h, rows):
                 nc.vector.quantize_mx(
                     out=probs_codes[:, h, rows].bitcast(FP8X4),
                     scales=probs_scales[:, h, rows],
@@ -398,16 +397,19 @@ def tile_treemodel_k_kernel(tc, x, W_gate, b_gate, leaf_logits_words, leaf_logit
                     go_right(f_9[:, 1, u, 1, half_rows[half]], acc_late[half][:, u, :], 1, 2 * u + 1)
                     go_left(f_9[:, 1, u, 0, half_rows[half]], f_9[:, 1, u, 1, half_rows[half]])
 
-            multiply_leaves(0, 0)
-            multiply_leaves(0, 1)
-            quantise_leaves(0, 0)
+            tile_rows = [slice(bt * P, (bt + 1) * P) for bt in range(BATCH_TILES)]
+            multiply_leaves(0, half_rows[0])
+            multiply_leaves(0, half_rows[1])
+            quantise_leaves(0, half_rows[0])
             late_branches(0)
-            multiply_leaves(1, 0)
-            quantise_leaves(0, 1)
-            quantise_leaves(1, 0)
+            multiply_leaves(1, half_rows[0])
+            quantise_leaves(0, half_rows[1])
+            quantise_leaves(1, half_rows[0])
             late_branches(1)
-            multiply_leaves(1, 1)
-            quantise_leaves(1, 1)
+            multiply_leaves(1, tile_rows[2])
+            multiply_leaves(1, tile_rows[3])
+            quantise_leaves(1, tile_rows[2])
+            quantise_leaves(1, tile_rows[3])
 
             for half in range(2):
                 acc_out = {}
@@ -427,7 +429,10 @@ def tile_treemodel_k_kernel(tc, x, W_gate, b_gate, leaf_logits_words, leaf_logit
                             )
                 for bt in range(2 * half, 2 * half + 2):
                     out_sb = result.tile([P, CLASSES], F32, name="out_sb")
-                    nc.vector.tensor_copy(out=out_sb[:, 0:N_TILE], in_=acc_out[(bt, 0)][:])
+                    if bt == 0:
+                        nc.scalar.copy(out=out_sb[:, 0:N_TILE], in_=acc_out[(bt, 0)][:])
+                    else:
+                        nc.vector.tensor_copy(out=out_sb[:, 0:N_TILE], in_=acc_out[(bt, 0)][:])
                     nc.sync.dma_start(out=out[bt * P : (bt + 1) * P, 0:N_TILE], in_=out_sb[:, 0:N_TILE])
                     nc.scalar.copy(out=out_sb[:, N_TILE:CLASSES], in_=acc_out[(bt, 1)][:])
                     nc.scalar.dma_start(out=out[bt * P : (bt + 1) * P, N_TILE:CLASSES], in_=out_sb[:, N_TILE:CLASSES])

@@ -275,21 +275,21 @@ def tile_treemodel_k_kernel(tc, x, W_gate, b_gate, leaf_logits_words, leaf_logit
             src, dst = every_2nd_node(last, 0)
             for u in range(2):
                 nc.scalar.copy(out=dst[:, u], in_=src[:, u])
+            src, dst = every_2nd_node(last, 1)
+            for u in range(2):
+                nc.vector.tensor_copy(out=dst[:, u], in_=src[:, u])
             multiply_plain(last)
             multiply_mx(last - 1, streamed[0:3])
             go_right(f_top[:, 1, :], acc_top[:], 0, 0)
             go_left(f_top[:, 0, :], f_top[:, 1, :])
             multiply_mx(last, streamed[0:3])
             quantise_w(last, 0, 2 * P, w_codes[last][:, 0 : 2 * P], w_scales[last][:, 0 : 2 * P])
+            quantise_w(last, 2 * P, 2 * P, late_codes[:, last, :], late_scales[:, last, :])
             turned_top = to_batch_rows(f_top, 6, "turned_top")
             multiply_mx(last - 1, streamed[3:5])
             multiply_mx(last, streamed[3:5])
-            src, dst = every_2nd_node(last, 1)
-            nc.scalar.copy(out=dst[:, 0], in_=src[:, 0])
             go_right(f_7[:, 1, :], acc_7[:], 0, 1)
             go_left(f_7[:, 0, :], f_7[:, 1, :])
-            nc.scalar.copy(out=dst[:, 1], in_=src[:, 1])
-            quantise_w(last, 2 * P, 2 * P, late_codes[:, last, :], late_scales[:, last, :])
 
             for q4 in range(4):
                 nc.sync.dma_start(
@@ -332,22 +332,22 @@ def tile_treemodel_k_kernel(tc, x, W_gate, b_gate, leaf_logits_words, leaf_logit
                 go_right(f_9[:, 0, u, 1, :], acc_9[u][:], 1, 2 * u)
             go_left(f_9[:, 0, :, 0, :], f_9[:, 0, :, 1, :])
 
-            probs = []
-            for pair in range(2):
-                root = tree.tile([P, 2, 1], F32, name="probs_0_%d" % pair)
-                nc.vector.memset(root[:], 1.0)
-                probs.append(root)
+            probs = [None, None]
             for level in range(8):
                 n = 2**level
                 turned, first = (turned_top, n - 1) if level < 7 else (turned_7, 0)
                 for pair in range(2):
                     children = tree.tile([P, 2, 2 * n], F32, name="probs_%d_%d" % (level + 1, pair))
-                    nc.vector.tensor_tensor(
-                        out=children[:].rearrange("p a (j s) -> p a j s", s=2),
-                        in0=turned[pair][:, :, :, first : first + n].rearrange("p a s j -> p a j s"),
-                        in1=probs[pair][:].unsqueeze(3).to_broadcast([P, 2, n, 2]),
-                        op=MULT,
-                    )
+                    branches = turned[pair][:, :, :, first : first + n].rearrange("p a s j -> p a j s")
+                    if level == 0:
+                        nc.vector.tensor_copy(out=children[:].rearrange("p a (j s) -> p a j s", s=2), in_=branches)
+                    else:
+                        nc.vector.tensor_tensor(
+                            out=children[:].rearrange("p a (j s) -> p a j s", s=2),
+                            in0=branches,
+                            in1=probs[pair][:].unsqueeze(3).to_broadcast([P, 2, n, 2]),
+                            op=MULT,
+                        )
                     probs[pair] = children
 
             late_passes(LATE_RUN, LATE_RUN)

import concourse.mybir as mybir
from concourse.masks import make_identity

F32 = mybir.dt.float32
BF16 = mybir.dt.bfloat16
I32 = mybir.dt.int32
U32 = mybir.dt.uint32
U8 = mybir.dt.uint8
FP8X4 = mybir.dt.float8_e4m3fn_x4
SIGMOID = mybir.ActivationFunctionType.Sigmoid
COPY = mybir.ActivationFunctionType.Copy
MULT = mybir.AluOpType.mult

P = 128
BATCH = 512
FEATURES = 8192
NODES = 1023
CLASSES = 1024
BATCH_TILES = BATCH // P
HALF_BATCH = BATCH // 2
K_PASS = 4 * P
PASSES = FEATURES // K_PASS
X_COLS = 1024
PASSES_PER_X = X_COLS // K_PASS
N_TILE = 512
W_RUN_PITCH = 2048

FIRST_7 = 127
FIRST_9 = 511
LATE_PASSES = 4 * PASSES
LATE_RUN = 12
OUT_BANKS = (0, 1, 4, 5, 6, 7, 2, 3)
SHARED_CUT = 16

FLOPS = 2 * BATCH * FEATURES * NODES + 2 * BATCH * CLASSES * CLASSES


def tile_treemodel_k_kernel(tc, x, W_gate, b_gate, leaf_logits_words, leaf_logits_scales, out):
    nc = tc.nc
    with tc.tile_pool(name="keep", bufs=1) as keep, tc.psum_pool(
        name="psum", bufs=1
    ) as psum, tc.manual_schedule():

        def bank(index, shape, name):
            return psum.tile(shape, F32, name=name, tag="bank%d" % index)

        ident = keep.tile([P, P], F32, name="ident")
        make_identity(nc, ident[:])

        leaf_codes = keep.tile([P, 2, 4 * CLASSES], U8, name="leaf_codes", align_bytes=64)
        leaf_scales = keep.tile([P, 2, CLASSES], U8, name="leaf_scales", align_bytes=64)
        nc.vector.memset(leaf_scales[:].bitcast(I32), 0)

        rows_plain = keep.tile([P, P], BF16, name="rows_plain")
        rows_every_2nd = keep.tile([P, 2 * P], BF16, name="rows_every_2nd")
        nc.vector.memset(rows_plain[:], 0.0)
        nc.vector.memset(rows_every_2nd[:], 0.0)
        nc.scalar.dma_start(out=rows_plain[0:1, :], in_=b_gate[0:P].unsqueeze(0))
        nc.scalar.dma_start(
            out=rows_plain[1:4, :], in_=b_gate[FIRST_7:FIRST_9].rearrange("(r n) -> r n", r=3)
        )
        nc.scalar.dma_start(
            out=rows_every_2nd[0:2, :], in_=b_gate[FIRST_9:NODES].rearrange("(r n) -> r n", r=2)
        )
        nc.scalar.dma_start(
            out=rows_every_2nd[2:3, :], in_=b_gate[FIRST_9 + 1 : FIRST_9 + 1 + 2 * P].unsqueeze(0)
        )
        nc.scalar.dma_start(
            out=rows_every_2nd[3:4, 0 : 2 * P - 1], in_=b_gate[FIRST_9 + 1 + 2 * P : NODES].unsqueeze(0)
        )
        table_warm = keep.tile([P, 1], F32, name="table_warm")
        nc.vector.memset(table_warm[:], 0.0)
        nc.scalar.activation(out=table_warm[:], in_=table_warm[:], func=SIGMOID)

        bias = keep.tile([P, 2, 4], F32, name="bias")

        def bias_to_partitions():
            rows_f32 = keep.tile([P, 2, P], F32, name="rows_f32")
            nc.vector.tensor_copy(out=rows_f32[:, 0, :], in_=rows_plain[:])
            nc.vector.tensor_copy(
                out=rows_f32[:, 1, :], in_=rows_every_2nd[:].rearrange("p (m two) -> p m two", two=2)[:, :, 0]
            )
            bias_ps = bank(1, [P, 2, P], "bias_ps")
            for i in range(2):
                nc.tensor.transpose(bias_ps[:, i, :], rows_f32[:, i, :], ident[:])
            nc.vector.tensor_copy(out=bias[:], in_=bias_ps[:, :, 0:4])

        def go_right(dst, logits, row, col):
            nc.scalar.activation(
                out=dst, in_=logits, func=SIGMOID, bias=bias[:, row, col : col + 1], scale=1.0
            )

        def go_left(dst, right):
            nc.scalar.activation(out=dst, in_=right, func=COPY, bias=1.0, scale=-1.0)

        def to_batch_rows(src, first_bank, name):
            turned = []
            for pair in range(2):
                ps = bank(first_bank + pair, [P, 2, 2, P], "%s%d" % (name, pair))
                for a in range(2):
                    bt = 2 * pair + a
                    for side in range(2):
                        nc.tensor.transpose(ps[:, a, side, :], src[:, side, bt * P : (bt + 1) * P], ident[:])
                turned.append(ps)
            return turned

        x_codes = keep.tile([P, PASSES, BATCH], U32, name="x_codes", align_bytes=64)
        x_scales = keep.tile([P, PASSES, BATCH], U8, name="x_scales", align_bytes=64)
        late_codes = keep.tile([P, PASSES, 2 * P], U32, name="late_codes", align_bytes=64)
        late_scales = keep.tile([P, PASSES, 2 * P], U8, name="late_scales", align_bytes=64)
        f_top = keep.tile([P, 2, BATCH], F32, name="f_top")
        f_7 = keep.tile([P, 2, BATCH], F32, name="f_7")

        acc_top = bank(0, [P, BATCH], "acc_top")

        with tc.tile_pool(name="x_raw", bufs=3 * BATCH_TILES) as x_pool, tc.tile_pool(
            name="w_raw", bufs=4
        ) as w_pool, tc.tile_pool(name="stage", bufs=2) as stage, tc.tile_pool(name="codes", bufs=3) as codes_pool:
            x_raw = {}
            x_t = {}
            x_grouped = {}
            w_raw = {}
            w_grouped = {}
            w_codes = {}
            w_scales = {}

            def load_x(block):
                for bt in range(BATCH_TILES):
                    x_raw[(block, bt)] = x_pool.tile([P, X_COLS], BF16, name="x_piece")
                    nc.sync.dma_start(
                        out=x_raw[(block, bt)][:],
                        in_=x[bt * P : (bt + 1) * P, block * X_COLS : (block + 1) * X_COLS],
                    )

            def load_w(c):
                w_tile = w_pool.tile([P, 2, W_RUN_PITCH], BF16, name="w_raw")
                w_raw[c] = w_tile[:, :, 0 : 2 * NODES].rearrange("p u (e n) -> p u e n", e=2)
                nc.sync.dma_start(
                    out=w_raw[c],
                    in_=W_gate[c * K_PASS : (c + 1) * K_PASS, :].rearrange("(u p e) n -> p u e n", u=2, p=P),
                )

            def transpose_x(c):
                block, c_in_block = divmod(c, PASSES_PER_X)
                x_t[c] = stage.tile([P, 2, BATCH], F32, name="x_t")
                for u in range(2):
                    xt_ps = bank(6 + u, [P, BATCH], "xt_ps%d" % u)
                    first = (2 * c_in_block + u) * P
                    for bt in range(BATCH_TILES):
                        nc.tensor.transpose(
                            xt_ps[:, bt * P : (bt + 1) * P],
                            x_raw[(block, bt)][:].bitcast(F32)[:, first : first + P],
                            ident[:],
                        )
                    nc.scalar.copy(out=x_t[c][:, u, :], in_=xt_ps[:])

            def group_x(c):
                x_grouped[c] = stage.tile([P, BATCH, 2], F32, name="x_grouped", align_bytes=64)
                nc.vector.tensor_copy(out=x_grouped[c][:], in_=x_t[c][:].rearrange("p u b -> p b u"))

            def quantise_x(c):
                nc.vector.quantize_mx(
                    out=x_codes[:, c, :].bitcast(FP8X4),
                    scales=x_scales[:, c, :],
                    in_=x_grouped[c][:].rearrange("p b u -> p (b u)").bitcast(BF16),
                )

            def every_2nd_node(c, h):
                first = FIRST_9 + 2 * P * h
                return (
                    w_raw[c][:, :, :, first : first + 2 * P].rearrange("p a e (mo i u) -> p u mo a e i", i=4, u=2),
                    w_grouped[c][:, 2 * P * h : 2 * P * (h + 1), :].rearrange(
                        "p (u mo i) (a e) -> p u mo a e i", u=2, i=4, a=2
                    ),
                )

            def group_w_on_vector(c):
                w_grouped[c] = stage.tile([P, 7 * P, 4], BF16, name="w_grouped", align_bytes=64)
                for h, u in ((0, 0), (0, 1), (1, 0)):
                    src, dst = every_2nd_node(c, h)
                    nc.vector.tensor_copy(out=dst[:, u], in_=src[:, u])
                src, dst = every_2nd_node(c, 1)
                nc.vector.tensor_copy(out=dst[:, 1, 0:SHARED_CUT], in_=src[:, 1, 0:SHARED_CUT])

            def group_w_on_scalar(c):
                src, dst = every_2nd_node(c, 1)
                nc.scalar.copy(out=dst[:, 1, SHARED_CUT:], in_=src[:, 1, SHARED_CUT:])
                nc.scalar.copy(
                    out=w_grouped[c][:, 4 * P : 7 * P, :].rearrange("p (no i) (a e) -> p no a e i", i=4, a=2),
                    in_=w_raw[c][:, :, :, FIRST_7:FIRST_9].rearrange("p a e (no i) -> p no a e i", i=4),
                )

            def quantise_w(c, first, count, codes, scales):
                nc.vector.quantize_mx(
                    out=codes.bitcast(FP8X4),
                    scales=scales,
                    in_=w_grouped[c][:, first : first + count, :].rearrange("p n t -> p (n t)"),
                )

            def quantise_w_from_vector(c):
                w_codes[c] = codes_pool.tile([P, 5 * P], U32, name="w_codes", align_bytes=64)
                w_scales[c] = codes_pool.tile([P, 5 * P], U8, name="w_scales", align_bytes=64)
                quantise_w(c, 0, 2 * P, w_codes[c][:, 0 : 2 * P], w_scales[c][:, 0 : 2 * P])

            def quantise_w_from_scalar(c):
                quantise_w(c, 2 * P, 2 * P, late_codes[:, c, :], late_scales[:, c, :])
                quantise_w(c, 4 * P, P, w_codes[c][:, 2 * P : 3 * P], w_scales[c][:, 2 * P : 3 * P])
                quantise_w(c, 5 * P, 2 * P, w_codes[c][:, 3 * P : 5 * P], w_scales[c][:, 3 * P : 5 * P])

            def multiply_plain(c):
                x_bf16 = x_t[c][:].bitcast(BF16).rearrange("p u (b e) -> p u b e", e=2)
                for t in range(4):
                    nc.tensor.matmul(
                        out=acc_top[:],
                        lhsT=w_raw[c][:, t // 2, t % 2, 0:P],
                        rhs=x_bf16[:, t // 2, :, t % 2],
                        start=(c == 0 and t == 0),
                        stop=(c == PASSES - 1 and t == 3),
                    )

            def multiply_mx(c, tiles):
                for acc, first in tiles:
                    nc.tensor.matmul_mx(
                        out=acc[:],
                        lhsT=w_codes[c][:, first : first + P].bitcast(FP8X4),
                        lhsT_scale=w_scales[c][:, first : first + P],
                        rhs=x_codes[:, c, :].bitcast(FP8X4),
                        rhs_scale=x_scales[:, c, :],
                        start=(c == 0),
                        stop=(c == PASSES - 1),
                    )

            def step(s):
                if s + 2 < PASSES:
                    if (s + 2) % PASSES_PER_X == 0:
                        load_x((s + 2) // PASSES_PER_X)
                    transpose_x(s + 2)
                if s + 1 >= 0:
                    load_w(s + 1)
                    group_w_on_vector(s + 1)
                    group_w_on_scalar(s + 1)
                    quantise_x(s + 1)
                    quantise_w_from_vector(s + 1)
                if s + 2 < PASSES:
                    group_x(s + 2)
                if s + 1 >= 0:
                    quantise_w_from_scalar(s + 1)
                if s >= 0:
                    multiply_mx(s, streamed)
                if s + 1 >= 0:
                    multiply_plain(s + 1)

            step(-2)
            step(-1)
            bias_to_partitions()
            acc_7 = bank(1, [P, BATCH], "acc_7")
            acc_8 = [bank(2 + h, [P, BATCH], "acc_8_%d" % h) for h in range(2)]
            acc_9 = [bank(4 + u, [P, BATCH], "acc_9_%d" % u) for u in range(2)]
            streamed = [(acc_7, 2 * P), (acc_8[0], 3 * P), (acc_8[1], 4 * P), (acc_9[0], 0), (acc_9[1], P)]
            for s in range(PASSES - 2):
                step(s)

            last = PASSES - 1
            load_w(last)
            w_grouped[last] = stage.tile([P, 7 * P, 4], BF16, name="w_grouped", align_bytes=64)
            w_codes[last] = codes_pool.tile([P, 5 * P], U32, name="w_codes", align_bytes=64)
            w_scales[last] = codes_pool.tile([P, 5 * P], U8, name="w_scales", align_bytes=64)
            nc.vector.tensor_copy(
                out=w_grouped[last][:, 4 * P : 7 * P, :].rearrange("p (no i) (a e) -> p no a e i", i=4, a=2),
                in_=w_raw[last][:, :, :, FIRST_7:FIRST_9].rearrange("p a e (no i) -> p no a e i", i=4),
            )
            quantise_x(last)
            quantise_w(last, 4 * P, P, w_codes[last][:, 2 * P : 3 * P], w_scales[last][:, 2 * P : 3 * P])
            quantise_w(last, 5 * P, 2 * P, w_codes[last][:, 3 * P : 5 * P], w_scales[last][:, 3 * P : 5 * P])
            src, dst = every_2nd_node(last, 0)
            for u in range(2):
                nc.scalar.copy(out=dst[:, u], in_=src[:, u])
            src, dst = every_2nd_node(last, 1)
            for u in range(2):
                nc.vector.tensor_copy(out=dst[:, u], in_=src[:, u])
            multiply_plain(last)
            multiply_mx(last - 1, streamed[0:3])
            go_right(f_top[:, 1, :], acc_top[:], 0, 0)
            go_left(f_top[:, 0, :], f_top[:, 1, :])
            multiply_mx(last, streamed[0:3])
            quantise_w(last, 0, 2 * P, w_codes[last][:, 0 : 2 * P], w_scales[last][:, 0 : 2 * P])
            quantise_w(last, 2 * P, 2 * P, late_codes[:, last, :], late_scales[:, last, :])
            turned_top = to_batch_rows(f_top, 6, "turned_top")
            multiply_mx(last - 1, streamed[3:5])
            multiply_mx(last, streamed[3:5])
            go_right(f_7[:, 1, :], acc_7[:], 0, 1)
            go_left(f_7[:, 0, :], f_7[:, 1, :])

            for q4 in range(4):
                nc.sync.dma_start(
                    out=leaf_scales[32 * q4 : 32 * q4 + 4, :, :].bitcast(I32),
                    in_=leaf_logits_scales[:, 4 * q4 : 4 * q4 + 4, :].bitcast(I32).rearrange("h r n -> r h n"),
                )
            for h in range(2):
                nc.sync.dma_start(
                    out=leaf_codes[:, h, :].bitcast(I32),
                    in_=leaf_logits_words[h].rearrange("p n t -> p (n t)").bitcast(I32),
                )

        with tc.tile_pool(name="tree", bufs=1) as tree, tc.tile_pool(name="result", bufs=BATCH_TILES) as result:
            acc_late = []

            def late_passes(first, count):
                for i in range(first, first + count):
                    half, u, c = i // (2 * PASSES), (i // PASSES) % 2, i % PASSES
                    rows = slice(half * HALF_BATCH, (half + 1) * HALF_BATCH)
                    nc.tensor.matmul_mx(
                        out=acc_late[half][:, u, :],
                        lhsT=late_codes[:, c, u * P : (u + 1) * P].bitcast(FP8X4),
                        lhsT_scale=late_scales[:, c, u * P : (u + 1) * P],
                        rhs=x_codes[:, c, rows].bitcast(FP8X4),
                        rhs_scale=x_scales[:, c, rows],
                        start=(c == 0),
                        stop=(c == PASSES - 1),
                    )

            f_8 = tree.tile([P, 2, 2, BATCH], F32, name="f_8")
            f_9 = tree.tile([P, 2, 2, 2, BATCH], F32, name="f_9")
            turned_7 = to_batch_rows(f_7, 0, "turned_7")
            for h in range(2):
                go_right(f_8[:, h, 1, :], acc_8[h][:], 0, 2 + h)
            for half in range(2):
                acc_late.append(bank(2 + half, [P, 2, HALF_BATCH], "acc_late%d" % half))
            late_passes(0, LATE_RUN)
            go_left(f_8[:, :, 0, :], f_8[:, :, 1, :])
            for u in range(2):
                go_right(f_9[:, 0, u, 1, :], acc_9[u][:], 1, 2 * u)
            go_left(f_9[:, 0, :, 0, :], f_9[:, 0, :, 1, :])

            probs = [None, None]
            for level in range(8):
                n = 2**level
                turned, first = (turned_top, n - 1) if level < 7 else (turned_7, 0)
                for pair in range(2):
                    children = tree.tile([P, 2, 2 * n], F32, name="probs_%d_%d" % (level + 1, pair))
                    branches = turned[pair][:, :, :, first : first + n].rearrange("p a s j -> p a j s")
                    if level == 0:
                        nc.vector.tensor_copy(out=children[:].rearrange("p a (j s) -> p a j s", s=2), in_=branches)
                    else:
                        nc.vector.tensor_tensor(
                            out=children[:].rearrange("p a (j s) -> p a j s", s=2),
                            in0=branches,
                            in1=probs[pair][:].unsqueeze(3).to_broadcast([P, 2, n, 2]),
                            op=MULT,
                        )
                    probs[pair] = children

            late_passes(LATE_RUN, LATE_RUN)
            into_8 = []
            for half in range(2):
                into_8.append(bank(6 + half, [P, 2, HALF_BATCH], "into_8_%d" % half))
                for h in range(2):
                    for a in range(2):
                        nc.tensor.transpose(
                            into_8[half][:, h, a * P : (a + 1) * P], probs[half][:, a, h * P : (h + 1) * P], ident[:]
                        )
            late_passes(2 * LATE_RUN, LATE_PASSES - 2 * LATE_RUN)

            into_9 = tree.tile([P, 2, 2, BATCH], F32, name="into_9")
            leaf_probs = tree.tile([P, 2, BATCH, 4], BF16, name="leaf_probs", align_bytes=64)
            probs_codes = tree.tile([P, 2, BATCH], U32, name="probs_codes", align_bytes=64)
            probs_scales = tree.tile([P, 2, BATCH], U8, name="probs_scales", align_bytes=64)
            half_rows = [slice(half * HALF_BATCH, (half + 1) * HALF_BATCH) for half in range(2)]
            for half in range(2):
                nc.vector.tensor_tensor(
                    out=into_9[:, :, :, half_rows[half]],
                    in0=into_8[half][:].unsqueeze(2).to_broadcast([P, 2, 2, HALF_BATCH]),
                    in1=f_8[:, :, :, half_rows[half]],
                    op=MULT,
                )

            def multiply_leaves(h, rows):
                nc.vector.tensor_tensor(
                    out=leaf_probs[:, h, rows, :].rearrange("p b (u e) -> p b u e", u=2),
                    in0=into_9[:, h, :, rows]
                    .rearrange("p u b -> p b u")
                    .unsqueeze(3)
                    .to_broadcast([P, rows.stop - rows.start, 2, 2]),
                    in1=f_9[:, h, :, :, rows].rearrange("p u e b -> p b u e"),
                    op=MULT,
                )

            def quantise_leaves(h, rows):
                nc.vector.quantize_mx(
                    out=probs_codes[:, h, rows].bitcast(FP8X4),
                    scales=probs_scales[:, h, rows],
                    in_=leaf_probs[:, h, rows, :].rearrange("p b t -> p (b t)"),
                )

            def late_branches(half):
                for u in range(2):
                    go_right(f_9[:, 1, u, 1, half_rows[half]], acc_late[half][:, u, :], 1, 2 * u + 1)
                    go_left(f_9[:, 1, u, 0, half_rows[half]], f_9[:, 1, u, 1, half_rows[half]])

            tile_rows = [slice(bt * P, (bt + 1) * P) for bt in range(BATCH_TILES)]
            multiply_leaves(0, half_rows[0])
            multiply_leaves(0, half_rows[1])
            quantise_leaves(0, half_rows[0])
            late_branches(0)
            multiply_leaves(1, half_rows[0])
            quantise_leaves(0, half_rows[1])
            quantise_leaves(1, half_rows[0])
            late_branches(1)
            multiply_leaves(1, tile_rows[2])
            multiply_leaves(1, tile_rows[3])
            quantise_leaves(1, tile_rows[2])
            quantise_leaves(1, tile_rows[3])

            for half in range(2):
                acc_out = {}
                for h in range(2):
                    for bt in range(2 * half, 2 * half + 2):
                        for n in range(CLASSES // N_TILE):
                            if h == 0:
                                acc_out[(bt, n)] = bank(OUT_BANKS[2 * bt + n], [P, N_TILE], "acc_out")
                            nc.tensor.matmul_mx(
                                out=acc_out[(bt, n)][:],
                                lhsT=probs_codes[:, h, bt * P : (bt + 1) * P].bitcast(FP8X4),
                                lhsT_scale=probs_scales[:, h, bt * P : (bt + 1) * P],
                                rhs=leaf_codes[:, h, 4 * N_TILE * n : 4 * N_TILE * (n + 1)].bitcast(FP8X4),
                                rhs_scale=leaf_scales[:, h, N_TILE * n : N_TILE * (n + 1)],
                                start=(h == 0),
                                stop=(h == 1),
                            )
                for bt in range(2 * half, 2 * half + 2):
                    out_sb = result.tile([P, CLASSES], F32, name="out_sb")
                    if bt == 0:
                        nc.scalar.copy(out=out_sb[:, 0:N_TILE], in_=acc_out[(bt, 0)][:])
                    else:
                        nc.vector.tensor_copy(out=out_sb[:, 0:N_TILE], in_=acc_out[(bt, 0)][:])
                    nc.sync.dma_start(out=out[bt * P : (bt + 1) * P, 0:N_TILE], in_=out_sb[:, 0:N_TILE])
                    nc.scalar.copy(out=out_sb[:, N_TILE:CLASSES], in_=acc_out[(bt, 1)][:])
                    nc.scalar.dma_start(out=out[bt * P : (bt + 1) * P, N_TILE:CLASSES], in_=out_sb[:, N_TILE:CLASSES])
